import numpy as np
import ml_dtypes


def mxq(x, axis, fmt="e4m3"):
    dtype, down = {"e4m3": (ml_dtypes.float8_e4m3fn, 7), "e5m2": (ml_dtypes.float8_e5m2, 14)}[fmt]
    v = np.moveaxis(np.asarray(x, np.float32).astype(ml_dtypes.bfloat16).astype(np.float64), axis, -1)
    blocks = v.reshape(v.shape[:-1] + (-1, 32))
    amax = np.abs(blocks).max(-1, keepdims=True)
    byte = np.maximum(np.where(amax > 0, np.frexp(amax)[1] - 1 + 127, 0) - down, 1)
    scale = np.exp2(byte - 127.0)
    codes = (blocks / scale).astype(np.float32).astype(dtype).astype(np.float64)
    return np.moveaxis((codes * scale).reshape(v.shape), -1, axis)


WIDE = False


def mx_kscale(k):
    if not WIDE:
        return np.ones(k)
    levels = np.array([10, -10, 5, -5, 0])
    a = np.random.permutation(np.resize(levels, k // 512 * 4)).reshape(k // 512, 4)
    idx = np.arange(k)
    return np.exp2(a[idx // 512, idx % 128 // 32])


BF16 = ml_dtypes.bfloat16


def bf(x):
    return np.asarray(x, np.float32).astype(BF16)


def f64(x):
    return np.asarray(x).astype(np.float64)


B, N, SIZE, CH = 4096, 16, 512, 256


def sigmoid(v):
    return 1.0 / (1.0 + np.exp(-v))


def setup_inputs():
    s = mx_kscale(SIZE)
    d = {"z0": bf(np.random.standard_normal((B, SIZE)) * s),
         "h_tilde": bf(np.random.standard_normal((B, CH)) * np.sqrt(N)),
         "fc_sum": bf(np.random.standard_normal((B, CH)) * 1.2)}
    for g in ("i", "o", "u"):
        d["W_" + g] = bf(np.random.standard_normal((CH, SIZE)) / np.sqrt(SIZE) / s)
        d["U_" + g] = bf(np.random.standard_normal((CH, CH)) / np.sqrt(CH * N))
        d["b_" + g] = bf(np.random.standard_normal(CH) * 0.5)
    return d


def reference(z0, h_tilde, fc_sum, W_i, U_i, b_i, W_o, U_o, b_o, W_u, U_u, b_u):
    zq = mxq(f64(z0), 1, "e4m3")
    ht = f64(h_tilde)
    i_j = sigmoid((zq @ mxq(f64(W_i), 1, "e4m3").T) + ht @ f64(U_i).T + f64(b_i))
    o_j = sigmoid((zq @ mxq(f64(W_o), 1, "e4m3").T) + ht @ f64(U_o).T + f64(b_o))
    u_j = np.tanh((zq @ mxq(f64(W_u), 1, "e4m3").T) + ht @ f64(U_u).T + f64(b_u))
    c_j = i_j * u_j + f64(fc_sum)
    h_j = o_j * np.tanh(c_j)
    return np.concatenate([h_j, c_j], axis=-1)

@@ -1,0 +1,327 @@
+from contextlib import ExitStack
+
+import concourse.bass as bass
+import concourse.mybir as mybir
+import concourse.tile as tile
+from concourse.masks import make_identity
+
+F32 = mybir.dt.float32
+BF16 = mybir.dt.bfloat16
+U32 = mybir.dt.uint32
+U8 = mybir.dt.uint8
+I32 = mybir.dt.int32
+FP8X4 = mybir.dt.float8_e4m3fn_x4
+ACT = mybir.ActivationFunctionType
+ALU = mybir.AluOpType
+
+P = 128
+B, SIZE, CH = 4096, 512, 256
+SLOTS = B // P
+GT = 4
+NG = SLOTS // GT
+NPAIR = 2 * NG
+FLOPS = 2 * B * (SIZE + CH) * 3 * CH
+MANUAL = True
+LAG = 4
+
+
+def tile_treelstm_pb_t_kernel(
+    tc, z0, h_tilde, fc_sum, W_i, U_i, b_i, W_o, U_o, b_o, W_u, U_u, b_u, out
+):
+    nc = tc.nc
+    with ExitStack() as ctx:
+        if MANUAL:
+            ctx.enter_context(tc.manual_schedule())
+        const = ctx.enter_context(tc.tile_pool(name="const", bufs=1))
+        front = ctx.enter_context(tc.tile_pool(name="front", bufs=2))
+        pio_pool = ctx.enter_context(tc.tile_pool(name="pio", bufs=5))
+        pu_pool = ctx.enter_context(tc.tile_pool(name="pu", bufs=3))
+        o_pool = ctx.enter_context(tc.tile_pool(name="osb", bufs=4))
+        tc_pool = ctx.enter_context(tc.tile_pool(name="tcn", bufs=3))
+        ps_t = ctx.enter_context(tc.psum_pool(name="pst", bufs=3))
+        ps_r = ctx.enter_context(tc.psum_pool(name="psr", bufs=5))
+
+        z0v = z0.rearrange("(p t) k -> p t k", t=SLOTS)
+        hv = h_tilde.rearrange("(p t) k -> p t k", t=SLOTS)
+        fv = fc_sum.rearrange("(p t) k -> p t k", t=SLOTS)
+        ov = out.rearrange("(p t) c -> p t c", t=SLOTS)
+
+        ident = const.tile([P, P], F32, name="ident")
+        make_identity(nc, ident[:])
+        ones = const.tile([P, P], BF16, name="ones")
+        nc.vector.memset(ones[:], 1.0)
+        brow = const.tile([P, 1024], BF16, name="brow")
+        nc.vector.memset(brow[:].bitcast(I32), 0)
+        warm = const.tile([P, 8], F32, name="warm")
+        nc.vector.memset(warm[:], 0.0)
+
+        for j, b in enumerate((b_i, b_o, b_u, b_u)):
+            nc.scalar.dma_start(
+                out=brow[0:1, 256 * j : 256 * (j + 1)],
+                in_=b.rearrange("(o n) -> o n", o=1),
+            )
+        nc.scalar.activation(out=warm[:], in_=warm[:], func=ACT.Sigmoid)
+
+        z_sb = [const.tile([P, GT, SIZE], BF16, name="z%d" % g) for g in range(NG)]
+        h_sb = [const.tile([P, GT, CH], BF16, name="h%d" % g) for g in range(NG)]
+        f_sb = [const.tile([P, GT, CH], BF16, name="f%d" % g) for g in range(NG)]
+        w_sb = [const.tile([P, 2, SIZE], BF16, name="w%d" % j) for j in range(3)]
+        u_sb = [const.tile([P, 2, CH], BF16, name="u%d" % j) for j in range(3)]
+
+        def load(dst, src, g):
+            nc.sync.dma_start(out=dst[g][:], in_=src[:, GT * g : GT * (g + 1), :])
+
+        load(h_sb, hv, 0)
+        for j, U in enumerate((U_i, U_o, U_u)):
+            nc.sync.dma_start(out=u_sb[j][:], in_=U.rearrange("(b p) k -> p b k", p=P))
+        load(z_sb, z0v, 0)
+        for j, W in enumerate((W_i, W_o, W_u)):
+            nc.sync.dma_start(out=w_sb[j][:], in_=W.rearrange("(b p) k -> p b k", p=P))
+        load(f_sb, fv, 0)
+        for g in range(1, NG):
+            load(z_sb, z0v, g)
+            load(h_sb, hv, g)
+            load(f_sb, fv, g)
+
+        st = {}
+
+        def transposes_h(g):
+            hf = h_sb[g][:].rearrange("p t k -> p (t k)").bitcast(F32)
+            th = ps_t.tile([P, 512], F32, name="th%d" % g, tag="T")
+            for t in range(GT):
+                nc.tensor.transpose(
+                    th[:, P * t : P * (t + 1)], hf[:, P * t : P * (t + 1)], ident[:]
+                )
+            st[("th", g)] = th
+
+        def transposes_z(g):
+            zf = z_sb[g][:].rearrange("p t k -> p (t k)").bitcast(F32)
+            tz = []
+            for q in range(2):
+                tzq = ps_t.tile([P, 512], F32, name="tz%d_%d" % (g, q), tag="T")
+                for s in range(2):
+                    for u in range(2):
+                        c = 256 * (2 * q + s) + P * u
+                        nc.tensor.transpose(
+                            tzq[:, 256 * s + P * u : 256 * s + P * (u + 1)],
+                            zf[:, c : c + P],
+                            ident[:],
+                        )
+                tz.append(tzq)
+            st[("tz", g)] = tz
+
+        def evacuate_h(g):
+            hT = front.tile([P, 512], F32, name="hT%d" % g, tag="hT")
+            nc.scalar.copy(out=hT[:], in_=st[("th", g)][:])
+            st[("hT", g)] = hT
+
+        def evacuate_z(g):
+            tz = st[("tz", g)]
+            gz = front.tile([P, 2048], BF16, name="gz%d" % g, tag="gz", align_bytes=64)
+            gzf = gz[:].bitcast(F32)
+            for q in range(2):
+                nc.scalar.copy(
+                    out=gzf[:, 512 * q : 512 * (q + 1)].rearrange(
+                        "p (s m u) -> p s m u", s=2, m=P, u=2
+                    ),
+                    in_=tz[q][:].rearrange("p (s u m) -> p s m u", s=2, u=2, m=P),
+                )
+            st[("gz", g)] = gz
+
+        def transposes(g):
+            transposes_h(g)
+            transposes_z(g)
+
+        def evacuate(g):
+            evacuate_h(g)
+            evacuate_z(g)
+
+        def quantise(g):
+            gz = st[("gz", g)]
+            zc = front.tile([P, 512], U32, name="zc%d" % g, tag="zc", align_bytes=64)
+            zs = front.tile([P, 512], U8, name="zs%d" % g, tag="zs", align_bytes=64)
+            nc.vector.quantize_mx(out=zc[:].bitcast(FP8X4), scales=zs[:], in_=gz[:])
+            st[("zc", g)] = (zc, zs)
+
+        transposes_h(0)
+        UTw = const.tile([P, 768], F32, name="UTw")
+        tuA = ps_r.tile([P, 512], F32, name="tuA", tag="R")
+        tuB = ps_r.tile([P, 512], F32, name="tuB", tag="R")
+        for j in range(3):
+            uf = u_sb[j][:].rearrange("p b k -> p (b k)").bitcast(F32)
+            for b in range(2):
+                dst = tuA[:, 256 * j + P * b : 256 * j + P * (b + 1)] if j < 2 else tuB[:, P * b : P * (b + 1)]
+                nc.tensor.transpose(dst, uf[:, P * b : P * (b + 1)], ident[:])
+        bias = const.tile([P, 1024], F32, name="bias")
+        pb = []
+        for j in range(2):
+            pbj = ps_r.tile([P, 512], F32, name="pb%d" % j, tag="R")
+            nc.tensor.matmul(
+                out=pbj[:], lhsT=ones[:], rhs=brow[:, 512 * j : 512 * (j + 1)], start=True, stop=True
+            )
+            pb.append(pbj)
+        transposes_z(0)
+        evacuate_h(0)
+        nc.scalar.copy(out=UTw[:, 0:512], in_=tuA[:])
+        nc.scalar.copy(out=UTw[:, 512:768], in_=tuB[:, 0:256])
+        for j in range(2):
+            nc.scalar.copy(out=bias[:, 512 * j : 512 * (j + 1)], in_=pb[j][:])
+        evacuate_z(0)
+        quantise(0)
+
+        gw = const.tile([P, 3072], BF16, name="gw", align_bytes=64)
+        gwf = gw[:].bitcast(F32)
+        wc = const.tile([P, 768], U32, name="wc", align_bytes=64)
+        ws = const.tile([P, 768], U8, name="ws", align_bytes=64)
+        for j in range(3):
+            wf = w_sb[j][:].rearrange("p b k -> p (b k)").bitcast(F32)
+            tw = ps_r.tile([P, 512], F32, name="tw%d" % j, tag="R")
+            for b in range(2):
+                for u in range(2):
+                    nc.tensor.transpose(
+                        tw[:, 256 * b + P * u : 256 * b + P * (u + 1)],
+                        wf[:, 256 * b + P * u : 256 * b + P * (u + 1)],
+                        ident[:],
+                    )
+            nc.scalar.copy(
+                out=gwf[:, 512 * j : 512 * (j + 1)].rearrange("p (s m u) -> p s m u", s=2, m=P, u=2),
+                in_=tw[:].rearrange("p (s u m) -> p s m u", s=2, u=2, m=P),
+            )
+        nc.vector.quantize_mx(out=wc[:, 0:512].bitcast(FP8X4), scales=ws[:, 0:512], in_=gw[:, 0:2048])
+        nc.vector.quantize_mx(out=wc[:, 512:768].bitcast(FP8X4), scales=ws[:, 512:768], in_=gw[:, 2048:3072])
+        UT = UTw[:].bitcast(BF16).rearrange("p (n e) -> p n e", e=2)
+
+        def pe_bank(n):
+            pr, k = divmod(n, 6)
+            g, q = divmod(pr, 2)
+            r = ps_r.tile([P, 512], F32, name="r%d" % n, tag="R")
+            st[("r", n)] = r
+            kk = k % 3
+            if kk < 2:
+                parts = [(2 * q + kk, 0, 512, 0)]
+            else:
+                parts = [(2 * q, 512, 768, 0), (2 * q + 1, 512, 768, 256)]
+            for t, c0, c1, o0 in parts:
+                dst = r[:, o0 : o0 + (c1 - c0)]
+                if k < 3:
+                    hT = st[("hT", g)][:].bitcast(BF16).rearrange("p (t m e) -> p t m e", t=GT, m=P, e=2)
+                    for e in range(2):
+                        nc.tensor.matmul(
+                            out=dst, lhsT=hT[:, t, :, e], rhs=UT[:, c0:c1, e], start=(e == 0), stop=(e == 1)
+                        )
+                else:
+                    zc, zs = st[("zc", g)]
+                    nc.tensor.matmul_mx(
+                        out=dst,
+                        lhsT=zc[:, P * t : P * (t + 1)].bitcast(FP8X4),
+                        lhsT_scale=zs[:, P * t : P * (t + 1)],
+                        rhs=wc[:, c0:c1].bitcast(FP8X4),
+                        rhs_scale=ws[:, c0:c1],
+                        start=True,
+                        stop=True,
+                    )
+
+        def pre_slice(g, q, kk):
+            if kk < 2:
+                return st[("pio", g)][:, 512 * (2 * q + kk) : 512 * (2 * q + kk + 1)]
+            return st[("pu", g)][:, 512 * q : 512 * (q + 1)]
+
+        def v_bank(n):
+            pr, k = divmod(n, 6)
+            g, q = divmod(pr, 2)
+            if q == 0 and k == 0:
+                st[("pio", g)] = pio_pool.tile([P, 2048], F32, name="pio%d" % g, tag="pio")
+                st[("pu", g)] = pu_pool.tile([P, 1024], F32, name="pu%d" % g, tag="pu")
+            kk = k % 3
+            dst = pre_slice(g, q, kk)
+            other = dst if k >= 3 else (bias[:, 0:512] if kk < 2 else bias[:, 512:1024])
+            nc.vector.tensor_tensor(out=dst, in0=st[("r", n)][:], in1=other, op=ALU.add)
+
+        def sig(pr):
+            g, q = divmod(pr, 2)
+            v = st[("pio", g)][:, 1024 * q : 1024 * (q + 1)]
+            nc.scalar.activation(out=v, in_=v, func=ACT.Sigmoid)
+
+        def tanh_u(pr):
+            g, q = divmod(pr, 2)
+            v = st[("pu", g)][:, 512 * q : 512 * (q + 1)]
+            nc.scalar.activation(out=v, in_=v, func=ACT.Tanh)
+
+        def views(g, t0, t1):
+            io = st[("pio", g)][:].rearrange("p (t c) -> p t c", c=512)
+            uu = st[("pu", g)][:].rearrange("p (t c) -> p t c", c=256)
+            oo = st[("o", g)][:]
+            return (
+                io[:, t0:t1, 0:256],
+                io[:, t0:t1, 256:512],
+                uu[:, t0:t1, :],
+                oo[:, t0:t1, 0:256],
+                oo[:, t0:t1, 256:512],
+            )
+
+        def cell(g, eng, t0, t1):
+            if ("o", g) not in st:
+                st[("o", g)] = o_pool.tile([P, GT, 512], F32, name="o%d" % g, tag="o")
+            gi, go, gu, oh, oc = views(g, t0, t1)
+            eng.tensor_tensor(out=oc, in0=gi, in1=gu, op=ALU.mult)
+            eng.tensor_tensor(out=oc, in0=oc, in1=f_sb[g][:, t0:t1, :], op=ALU.add)
+
+        def tanh_c(g, t0, t1):
+            if ("tc", g) not in st:
+                st[("tc", g)] = tc_pool.tile([P, GT, 256], F32, name="tc%d" % g, tag="tc")
+            gi, go, gu, oh, oc = views(g, t0, t1)
+            nc.scalar.activation(out=st[("tc", g)][:, t0:t1, :], in_=oc, func=ACT.Tanh)
+
+        def hidden(g, eng, t0, t1):
+            gi, go, gu, oh, oc = views(g, t0, t1)
+            eng.tensor_tensor(out=oh, in0=go, in1=st[("tc", g)][:, t0:t1, :], op=ALU.mult)
+
+        def store(g, t0, t1):
+            nc.sync.dma_start(out=ov[:, GT * g + t0 : GT * g + t1, :], in_=st[("o", g)][:, t0:t1, :])
+
+        NB = 6 * NPAIR
+        for n in range(NB + LAG):
+            if n < NB:
+                pe_bank(n)
+                pr, k = divmod(n, 6)
+                if k == 5:
+                    if pr == 0:
+                        transposes(1)
+                    elif pr % 2 == 1 and (pr + 3) // 2 < NG:
+                        transposes((pr + 3) // 2)
+            m = n - LAG
+            if m < 0:
+                continue
+            v_bank(m)
+            pr, k = divmod(m, 6)
+            g, q = divmod(pr, 2)
+            if pr == NPAIR - 1 and k == 2:
+                cell(NG - 1, nc.vector, 0, 2)
+                tanh_c(NG - 1, 0, 2)
+                tanh_c(NG - 2, 0, GT)
+            if pr == 1 and k == 4:
+                quantise(1)
+            if k == 4:
+                sig(pr)
+            if k == 5:
+                tanh_u(pr)
+                if pr == 0:
+                    evacuate(1)
+                elif q == 1 and (pr + 3) // 2 < NG:
+                    evacuate((pr + 3) // 2)
+                if q == 0 and 2 <= g + 1 < NG:
+                    quantise(g + 1)
+                if q == 1 and g < NG - 1:
+                    cell(g, nc.gpsimd, 0, GT)
+                if q == 0 and g - 2 >= 0:
+                    tanh_c(g - 2, 0, GT)
+                    hidden(g - 2, nc.gpsimd, 0, GT)
+                    store(g - 2, 0, GT)
+        hidden(NG - 2, nc.gpsimd, 0, GT)
+        store(NG - 2, 0, GT)
+        hidden(NG - 1, nc.vector, 0, 2)
+        store(NG - 1, 0, 2)
+        cell(NG - 1, nc.vector, 2, 4)
+        tanh_c(NG - 1, 2, 4)
+        hidden(NG - 1, nc.vector, 2, 4)
+        store(NG - 1, 2, 4)

@@ -1,8 +1,6 @@
 from contextlib import ExitStack
 
-import concourse.bass as bass
 import concourse.mybir as mybir
-import concourse.tile as tile
 from concourse.masks import make_identity
 
 F32 = mybir.dt.float32
@@ -23,6 +21,8 @@ NPAIR = 2 * NG
 FLOPS = 2 * B * (SIZE + CH) * 3 * CH
 MANUAL = True
 LAG = 4
+VU = 12
+FLAGGED = (2, 3, 5, 7, 9, 11, 12, 13, 14, 15)
 
 
 def tile_treelstm_pb_t_kernel(
@@ -46,20 +46,19 @@ def tile_treelstm_pb_t_kernel(
         fv = fc_sum.rearrange("(p t) k -> p t k", t=SLOTS)
         ov = out.rearrange("(p t) c -> p t c", t=SLOTS)
 
-        ident = const.tile([P, P], F32, name="ident")
-        make_identity(nc, ident[:])
-        ones = const.tile([P, P], BF16, name="ones")
-        nc.vector.memset(ones[:], 1.0)
-        brow = const.tile([P, 1024], BF16, name="brow")
+        brow = const.tile([P, 768], BF16, name="brow")
         nc.vector.memset(brow[:].bitcast(I32), 0)
-        warm = const.tile([P, 8], F32, name="warm")
-        nc.vector.memset(warm[:], 0.0)
-
-        for j, b in enumerate((b_i, b_o, b_u, b_u)):
+        for j, b in enumerate((b_i, b_o, b_u)):
             nc.scalar.dma_start(
                 out=brow[0:1, 256 * j : 256 * (j + 1)],
                 in_=b.rearrange("(o n) -> o n", o=1),
             )
+        ident = const.tile([P, P], F32, name="ident")
+        make_identity(nc, ident[:])
+        ones = const.tile([P, P], BF16, name="ones")
+        nc.vector.memset(ones[:], 1.0)
+        warm = const.tile([P, 8], F32, name="warm")
+        nc.vector.memset(warm[:], 0.0)
         nc.scalar.activation(out=warm[:], in_=warm[:], func=ACT.Sigmoid)
 
         z_sb = [const.tile([P, GT, SIZE], BF16, name="z%d" % g) for g in range(NG)]
@@ -68,15 +67,21 @@ def tile_treelstm_pb_t_kernel(
         w_sb = [const.tile([P, 2, SIZE], BF16, name="w%d" % j) for j in range(3)]
         u_sb = [const.tile([P, 2, CH], BF16, name="u%d" % j) for j in range(3)]
 
-        def load(dst, src, g):
-            nc.sync.dma_start(out=dst[g][:], in_=src[:, GT * g : GT * (g + 1), :])
+        def load(dst, src, g, t0=0, t1=GT):
+            nc.sync.dma_start(out=dst[g][:, t0:t1, :], in_=src[:, GT * g + t0 : GT * g + t1, :])
 
+        def load_w(dst, src):
+            nc.sync.dma_start(out=dst[:], in_=src.rearrange("(b p) k -> p b k", p=P))
+
+        load_w(u_sb[0], U_i)
+        load_w(u_sb[1], U_o)
         load(h_sb, hv, 0)
-        for j, U in enumerate((U_i, U_o, U_u)):
-            nc.sync.dma_start(out=u_sb[j][:], in_=U.rearrange("(b p) k -> p b k", p=P))
-        load(z_sb, z0v, 0)
-        for j, W in enumerate((W_i, W_o, W_u)):
-            nc.sync.dma_start(out=w_sb[j][:], in_=W.rearrange("(b p) k -> p b k", p=P))
+        load_w(u_sb[2], U_u)
+        load_w(w_sb[0], W_i)
+        load_w(w_sb[1], W_o)
+        load(z_sb, z0v, 0, 0, 2)
+        load_w(w_sb[2], W_u)
+        load(z_sb, z0v, 0, 2, 4)
         load(f_sb, fv, 0)
         for g in range(1, NG):
             load(z_sb, z0v, g)
@@ -89,114 +94,77 @@ def tile_treelstm_pb_t_kernel(
             hf = h_sb[g][:].rearrange("p t k -> p (t k)").bitcast(F32)
             th = ps_t.tile([P, 512], F32, name="th%d" % g, tag="T")
             for t in range(GT):
-                nc.tensor.transpose(
-                    th[:, P * t : P * (t + 1)], hf[:, P * t : P * (t + 1)], ident[:]
-                )
+                nc.tensor.transpose(th[:, P * t : P * (t + 1)], hf[:, P * t : P * (t + 1)], ident[:])
             st[("th", g)] = th
 
-        def transposes_z(g):
+        def transposes_z(g, q):
             zf = z_sb[g][:].rearrange("p t k -> p (t k)").bitcast(F32)
-            tz = []
-            for q in range(2):
-                tzq = ps_t.tile([P, 512], F32, name="tz%d_%d" % (g, q), tag="T")
-                for s in range(2):
-                    for u in range(2):
-                        c = 256 * (2 * q + s) + P * u
-                        nc.tensor.transpose(
-                            tzq[:, 256 * s + P * u : 256 * s + P * (u + 1)],
-                            zf[:, c : c + P],
-                            ident[:],
-                        )
-                tz.append(tzq)
-            st[("tz", g)] = tz
+            tzq = ps_t.tile([P, 512], F32, name="tz%d_%d" % (g, q), tag="T")
+            for s in range(2):
+                for u in range(2):
+                    c = 256 * (2 * q + s) + P * u
+                    nc.tensor.transpose(
+                        tzq[:, 256 * s + P * u : 256 * s + P * (u + 1)], zf[:, c : c + P], ident[:]
+                    )
+            st[("tz", g, q)] = tzq
 
-        def evacuate_h(g):
+        def evacuate_h(g, eng_copy):
             hT = front.tile([P, 512], F32, name="hT%d" % g, tag="hT")
-            nc.scalar.copy(out=hT[:], in_=st[("th", g)][:])
+            eng_copy(out=hT[:], in_=st[("th", g)][:])
             st[("hT", g)] = hT
 
-        def evacuate_z(g):
-            tz = st[("tz", g)]
-            gz = front.tile([P, 2048], BF16, name="gz%d" % g, tag="gz", align_bytes=64)
-            gzf = gz[:].bitcast(F32)
-            for q in range(2):
-                nc.scalar.copy(
-                    out=gzf[:, 512 * q : 512 * (q + 1)].rearrange(
-                        "p (s m u) -> p s m u", s=2, m=P, u=2
-                    ),
-                    in_=tz[q][:].rearrange("p (s u m) -> p s m u", s=2, u=2, m=P),
-                )
-            st[("gz", g)] = gz
+        def regroup(eng_copy, dst_f32, bank):
+            eng_copy(
+                out=dst_f32.rearrange("p (s m u) -> p s m u", s=2, m=P, u=2),
+                in_=bank[:].rearrange("p (s u m) -> p s m u", s=2, u=2, m=P),
+            )
+
+        def evacuate_z(g, q, eng_copy):
+            if q == 0:
+                st[("gz", g)] = front.tile([P, 2048], BF16, name="gz%d" % g, tag="gz", align_bytes=64)
+            gzf = st[("gz", g)][:].bitcast(F32)
+            regroup(eng_copy, gzf[:, 512 * q : 512 * (q + 1)], st[("tz", g, q)])
+
+        def quantise(g, q0, q1):
+            gz = st[("gz", g)]
+            if q0 == 0:
+                zc = front.tile([P, 512], U32, name="zc%d" % g, tag="zc", align_bytes=64)
+                zs = front.tile([P, 512], U8, name="zs%d" % g, tag="zs", align_bytes=64)
+                st[("zc", g)] = (zc, zs)
+            zc, zs = st[("zc", g)]
+            nc.vector.quantize_mx(
+                out=zc[:, 256 * q0 : 256 * q1].bitcast(FP8X4),
+                scales=zs[:, 256 * q0 : 256 * q1],
+                in_=gz[:, 1024 * q0 : 1024 * q1],
+            )
 
         def transposes(g):
             transposes_h(g)
-            transposes_z(g)
+            transposes_z(g, 0)
+            transposes_z(g, 1)
 
         def evacuate(g):
-            evacuate_h(g)
-            evacuate_z(g)
+            evacuate_h(g, nc.scalar.copy)
+            evacuate_z(g, 0, nc.scalar.copy)
+            evacuate_z(g, 1, nc.scalar.copy)
 
-        def quantise(g):
-            gz = st[("gz", g)]
-            zc = front.tile([P, 512], U32, name="zc%d" % g, tag="zc", align_bytes=64)
-            zs = front.tile([P, 512], U8, name="zs%d" % g, tag="zs", align_bytes=64)
-            nc.vector.quantize_mx(out=zc[:].bitcast(FP8X4), scales=zs[:], in_=gz[:])
-            st[("zc", g)] = (zc, zs)
-
-        transposes_h(0)
         UTw = const.tile([P, 768], F32, name="UTw")
-        tuA = ps_r.tile([P, 512], F32, name="tuA", tag="R")
-        tuB = ps_r.tile([P, 512], F32, name="tuB", tag="R")
-        for j in range(3):
-            uf = u_sb[j][:].rearrange("p b k -> p (b k)").bitcast(F32)
-            for b in range(2):
-                dst = tuA[:, 256 * j + P * b : 256 * j + P * (b + 1)] if j < 2 else tuB[:, P * b : P * (b + 1)]
-                nc.tensor.transpose(dst, uf[:, P * b : P * (b + 1)], ident[:])
+        UT = UTw[:].bitcast(BF16).rearrange("p (n e) -> p n e", e=2)
         bias = const.tile([P, 1024], F32, name="bias")
-        pb = []
-        for j in range(2):
-            pbj = ps_r.tile([P, 512], F32, name="pb%d" % j, tag="R")
-            nc.tensor.matmul(
-                out=pbj[:], lhsT=ones[:], rhs=brow[:, 512 * j : 512 * (j + 1)], start=True, stop=True
-            )
-            pb.append(pbj)
-        transposes_z(0)
-        evacuate_h(0)
-        nc.scalar.copy(out=UTw[:, 0:512], in_=tuA[:])
-        nc.scalar.copy(out=UTw[:, 512:768], in_=tuB[:, 0:256])
-        for j in range(2):
-            nc.scalar.copy(out=bias[:, 512 * j : 512 * (j + 1)], in_=pb[j][:])
-        evacuate_z(0)
-        quantise(0)
-
         gw = const.tile([P, 3072], BF16, name="gw", align_bytes=64)
         gwf = gw[:].bitcast(F32)
         wc = const.tile([P, 768], U32, name="wc", align_bytes=64)
         ws = const.tile([P, 768], U8, name="ws", align_bytes=64)
-        for j in range(3):
-            wf = w_sb[j][:].rearrange("p b k -> p (b k)").bitcast(F32)
-            tw = ps_r.tile([P, 512], F32, name="tw%d" % j, tag="R")
-            for b in range(2):
-                for u in range(2):
-                    nc.tensor.transpose(
-                        tw[:, 256 * b + P * u : 256 * b + P * (u + 1)],
-                        wf[:, 256 * b + P * u : 256 * b + P * (u + 1)],
-                        ident[:],
-                    )
-            nc.scalar.copy(
-                out=gwf[:, 512 * j : 512 * (j + 1)].rearrange("p (s m u) -> p s m u", s=2, m=P, u=2),
-                in_=tw[:].rearrange("p (s u m) -> p s m u", s=2, u=2, m=P),
-            )
-        nc.vector.quantize_mx(out=wc[:, 0:512].bitcast(FP8X4), scales=ws[:, 0:512], in_=gw[:, 0:2048])
-        nc.vector.quantize_mx(out=wc[:, 512:768].bitcast(FP8X4), scales=ws[:, 512:768], in_=gw[:, 2048:3072])
-        UT = UTw[:].bitcast(BF16).rearrange("p (n e) -> p n e", e=2)
+
+        def kk_of(pr, k):
+            return (0, 2, 1)[k % 3] if pr == NPAIR - 1 else k % 3
 
         def pe_bank(n):
             pr, k = divmod(n, 6)
             g, q = divmod(pr, 2)
             r = ps_r.tile([P, 512], F32, name="r%d" % n, tag="R")
             st[("r", n)] = r
-            kk = k % 3
+            kk = kk_of(pr, k)
             if kk < 2:
                 parts = [(2 * q + kk, 0, 512, 0)]
             else:
@@ -205,10 +173,17 @@ def tile_treelstm_pb_t_kernel(
                 dst = r[:, o0 : o0 + (c1 - c0)]
                 if k < 3:
                     hT = st[("hT", g)][:].bitcast(BF16).rearrange("p (t m e) -> p t m e", t=GT, m=P, e=2)
+                    pe_bias = kk == 2 and pr in FLAGGED
                     for e in range(2):
                         nc.tensor.matmul(
-                            out=dst, lhsT=hT[:, t, :, e], rhs=UT[:, c0:c1, e], start=(e == 0), stop=(e == 1)
+                            out=dst,
+                            lhsT=hT[:, t, :, e],
+                            rhs=UT[:, c0:c1, e],
+                            start=(e == 0),
+                            stop=(e == 1 and not pe_bias),
                         )
+                    if pe_bias:
+                        nc.tensor.matmul(out=dst, lhsT=ones[:], rhs=brow[:, c0:c1], start=False, stop=True)
                 else:
                     zc, zs = st[("zc", g)]
                     nc.tensor.matmul_mx(
@@ -226,25 +201,33 @@ def tile_treelstm_pb_t_kernel(
                 return st[("pio", g)][:, 512 * (2 * q + kk) : 512 * (2 * q + kk + 1)]
             return st[("pu", g)][:, 512 * q : 512 * (q + 1)]
 
+        def alloc_pre(g):
+            if ("pio", g) not in st:
+                st[("pio", g)] = pio_pool.tile([P, 2048], F32, name="pio%d" % g, tag="pio")
+                st[("pu", g)] = pu_pool.tile([P, 1024], F32, name="pu%d" % g, tag="pu")
+
         def v_bank(n):
             pr, k = divmod(n, 6)
             g, q = divmod(pr, 2)
-            if q == 0 and k == 0:
-                st[("pio", g)] = pio_pool.tile([P, 2048], F32, name="pio%d" % g, tag="pio")
-                st[("pu", g)] = pu_pool.tile([P, 1024], F32, name="pu%d" % g, tag="pu")
-            kk = k % 3
+            alloc_pre(g)
+            kk = kk_of(pr, k)
+            if k < 3 and kk == 2 and pr in FLAGGED:
+                return
             dst = pre_slice(g, q, kk)
             other = dst if k >= 3 else (bias[:, 0:512] if kk < 2 else bias[:, 512:1024])
             nc.vector.tensor_tensor(out=dst, in0=st[("r", n)][:], in1=other, op=ALU.add)
 
-        def sig(pr):
+        def s_bank(pr):
             g, q = divmod(pr, 2)
-            v = st[("pio", g)][:, 1024 * q : 1024 * (q + 1)]
+            alloc_pre(g)
+            nc.scalar.copy(out=pre_slice(g, q, 2), in_=st[("r", 6 * pr + (1 if pr == NPAIR - 1 else 2))][:])
+
+        def sig(g, t0, t1):
+            v = st[("pio", g)][:, 512 * t0 : 512 * t1]
             nc.scalar.activation(out=v, in_=v, func=ACT.Sigmoid)
 
-        def tanh_u(pr):
-            g, q = divmod(pr, 2)
-            v = st[("pu", g)][:, 512 * q : 512 * (q + 1)]
+        def tanh_u(g, t0, t1):
+            v = st[("pu", g)][:, 256 * t0 : 256 * t1]
             nc.scalar.activation(out=v, in_=v, func=ACT.Tanh)
 
         def views(g, t0, t1):
@@ -276,52 +259,134 @@ def tile_treelstm_pb_t_kernel(
             gi, go, gu, oh, oc = views(g, t0, t1)
             eng.tensor_tensor(out=oh, in0=go, in1=st[("tc", g)][:, t0:t1, :], op=ALU.mult)
 
-        def store(g, t0, t1):
-            nc.sync.dma_start(out=ov[:, GT * g + t0 : GT * g + t1, :], in_=st[("o", g)][:, t0:t1, :])
+        def store(g, t0, t1, c0=0, c1=512):
+            nc.sync.dma_start(
+                out=ov[:, GT * g + t0 : GT * g + t1, c0:c1], in_=st[("o", g)][:, t0:t1, c0:c1]
+            )
+
+        tuA = ps_r.tile([P, 512], F32, name="tuA", tag="R")
+        tuB = ps_r.tile([P, 512], F32, name="tuB", tag="R")
+
+        def transposes_u(j):
+            uf = u_sb[j][:].rearrange("p b k -> p (b k)").bitcast(F32)
+            for b in range(2):
+                dst = tuA[:, 256 * j + P * b : 256 * j + P * (b + 1)] if j < 2 else tuB[:, P * b : P * (b + 1)]
+                nc.tensor.transpose(dst, uf[:, P * b : P * (b + 1)], ident[:])
+
+        def transposes_w(j):
+            wf = w_sb[j][:].rearrange("p b k -> p (b k)").bitcast(F32)
+            tw = ps_r.tile([P, 512], F32, name="tw%d" % j, tag="R")
+            for c in range(4):
+                nc.tensor.transpose(tw[:, P * c : P * (c + 1)], wf[:, P * c : P * (c + 1)], ident[:])
+            st[("tw", j)] = tw
+
+        transposes_u(0)
+        transposes_u(1)
+        nc.vector.tensor_copy(out=UTw[:, 0:512], in_=tuA[:])
+        transposes_h(0)
+        evacuate_h(0, nc.scalar.copy)
+        transposes_u(2)
+        nc.vector.tensor_copy(out=UTw[:, 512:768], in_=tuB[:, 0:256])
+        pb0 = ps_r.tile([P, 512], F32, name="pb0", tag="R")
+        nc.tensor.matmul(out=pb0[:], lhsT=ones[:], rhs=brow[:, 0:512], start=True, stop=True)
+        pb1 = ps_r.tile([P, 512], F32, name="pb1", tag="R")
+        for j in range(2):
+            nc.tensor.matmul(
+                out=pb1[:, 256 * j : 256 * (j + 1)], lhsT=ones[:], rhs=brow[:, 512:768], start=True, stop=True
+            )
+        nc.scalar.copy(out=bias[:, 0:512], in_=pb0[:])
+        nc.vector.tensor_copy(out=bias[:, 512:1024], in_=pb1[:])
+        HEAD = (("pe", 0), ("v", 0), ("tw", 0), ("ew", 0, "s"), ("pe", 1), ("v", 1), ("tw", 1), ("ew", 1, "s"), ("tz", 0), ("ez", 0, "s"), ("pe", 2), ("v", 2), ("qw", 0), ("tw", 2), ("ew", 2, "s"), ("qz", 0), ("pe", 6), ("v", 6), ("qw", 1), ("tz", 1), ("ez", 1, "s"), ("pe", 7), ("v", 7), ("qz", 1), ("pe", 8), ("v", 8), ("T", 1), ("E", 1))
+        for step in HEAD:
+            if step[0] == "tw":
+                transposes_w(step[1])
+            elif step[0] == "ew":
+                regroup(
+                    nc.scalar.copy if step[2] == "s" else nc.vector.tensor_copy,
+                    gwf[:, 512 * step[1] : 512 * (step[1] + 1)],
+                    st[("tw", step[1])],
+                )
+            elif step[0] == "qw":
+                if step[1] == 0:
+                    nc.vector.quantize_mx(out=wc[:, 0:512].bitcast(FP8X4), scales=ws[:, 0:512], in_=gw[:, 0:2048])
+                else:
+                    nc.vector.quantize_mx(
+                        out=wc[:, 512:768].bitcast(FP8X4), scales=ws[:, 512:768], in_=gw[:, 2048:3072]
+                    )
+            elif step[0] == "tz":
+                transposes_z(0, step[1])
+            elif step[0] == "ez":
+                evacuate_z(0, step[1], nc.scalar.copy if step[2] == "s" else nc.vector.tensor_copy)
+            elif step[0] == "qz":
+                quantise(0, step[1], step[1] + 1)
+            elif step[0] == "T":
+                transposes(step[1])
+            elif step[0] == "E":
+                evacuate(step[1])
+            elif step[0] == "pe":
+                pe_bank(step[1])
+            elif step[0] == "v":
+                v_bank(step[1])
 
         NB = 6 * NPAIR
+        done_pe = set(s[1] for s in HEAD if s[0] == "pe")
+        done_v = set(s[1] for s in HEAD if s[0] == "v")
         for n in range(NB + LAG):
             if n < NB:
-                pe_bank(n)
+                if n not in done_pe:
+                    pe_bank(n)
                 pr, k = divmod(n, 6)
                 if k == 5:
-                    if pr == 0:
-                        transposes(1)
-                    elif pr % 2 == 1 and (pr + 3) // 2 < NG:
+                    if pr % 2 == 1 and (pr + 3) // 2 < NG:
                         transposes((pr + 3) // 2)
             m = n - LAG
             if m < 0:
                 continue
-            v_bank(m)
+            if m not in done_v:
+                v_bank(m)
             pr, k = divmod(m, 6)
             g, q = divmod(pr, 2)
-            if pr == NPAIR - 1 and k == 2:
-                cell(NG - 1, nc.vector, 0, 2)
-                tanh_c(NG - 1, 0, 2)
-                tanh_c(NG - 2, 0, GT)
+            if k == 2:
+                if pr - 2 >= VU:
+                    hidden((pr - 2) // 2, nc.vector, 2 * (pr % 2), 2 * (pr % 2) + 2)
+                    store((pr - 2) // 2, 2 * (pr % 2), 2 * (pr % 2) + 2)
+                if pr - 1 >= VU:
+                    cell((pr - 1) // 2, nc.vector, 2 * ((pr - 1) % 2), 2 * ((pr - 1) % 2) + 2)
+                    tanh_c((pr - 1) // 2, 2 * ((pr - 1) % 2), 2 * ((pr - 1) % 2) + 2)
             if pr == 1 and k == 4:
-                quantise(1)
+                quantise(1, 0, 2)
+            if pr == NPAIR - 1:
+                if k == 3:
+                    sig(g, 2, 3)
+                if k == 4:
+                    tanh_u(g, 2, 4)
+                if k == 5:
+                    sig(g, 3, 4)
+                continue
             if k == 4:
-                sig(pr)
+                sig(g, 2 * q, 2 * q + 2)
             if k == 5:
-                tanh_u(pr)
-                if pr == 0:
-                    evacuate(1)
-                elif q == 1 and (pr + 3) // 2 < NG:
+                tanh_u(g, 2 * q, 2 * q + 2)
+                if pr + 1 in FLAGGED:
+                    s_bank(pr + 1)
+                if q == 1 and (pr + 3) // 2 < NG:
                     evacuate((pr + 3) // 2)
                 if q == 0 and 2 <= g + 1 < NG:
-                    quantise(g + 1)
-                if q == 1 and g < NG - 1:
+                    quantise(g + 1, 0, 2)
+                if q == 1 and pr < VU:
                     cell(g, nc.gpsimd, 0, GT)
-                if q == 0 and g - 2 >= 0:
-                    tanh_c(g - 2, 0, GT)
-                    hidden(g - 2, nc.gpsimd, 0, GT)
-                    store(g - 2, 0, GT)
-        hidden(NG - 2, nc.gpsimd, 0, GT)
-        store(NG - 2, 0, GT)
+                for gg in range(VU // 2):
+                    if pr == min(2 * gg + 4, VU + 1):
+                        tanh_c(gg, 0, GT)
+                        hidden(gg, nc.gpsimd, 0, GT)
+                        store(gg, 0, GT)
+        cell(NG - 1, nc.vector, 2, 3)
+        tanh_c(NG - 1, 2, 3)
         hidden(NG - 1, nc.vector, 0, 2)
         store(NG - 1, 0, 2)
-        cell(NG - 1, nc.vector, 2, 4)
-        tanh_c(NG - 1, 2, 4)
-        hidden(NG - 1, nc.vector, 2, 4)
-        store(NG - 1, 2, 4)
+        cell(NG - 1, nc.vector, 3, 4)
+        tanh_c(NG - 1, 3, 4)
+        hidden(NG - 1, nc.vector, 2, 3)
+        store(NG - 1, 2, 3)
+        hidden(NG - 1, nc.vector, 3, 4)
+        store(NG - 1, 3, 4)

@@ -108,6 +108,39 @@ def tile_treelstm_pb_t_kernel(
                     )
             st[("tz", g, q)] = tzq
 
+        def one_h(g, t):
+            if t == 0:
+                st[("th", g)] = ps_t.tile([P, 512], F32, name="th%d" % g, tag="T")
+            hf = h_sb[g][:].rearrange("p t k -> p (t k)").bitcast(F32)
+            nc.tensor.transpose(st[("th", g)][:, P * t : P * (t + 1)], hf[:, P * t : P * (t + 1)], ident[:])
+
+        def one_z(g, q, j):
+            if j == 0:
+                st[("tz", g, q)] = ps_t.tile([P, 512], F32, name="tz%d_%d" % (g, q), tag="T")
+            zf = z_sb[g][:].rearrange("p t k -> p (t k)").bitcast(F32)
+            nc.tensor.transpose(
+                st[("tz", g, q)][:, P * j : P * (j + 1)], zf[:, 512 * q + P * j : 512 * q + P * (j + 1)], ident[:]
+            )
+
+        def woven(pr):
+            g = (pr + 3) // 2
+            if pr < 2 or g >= NG:
+                return []
+            first = [("h", g, 0, t) for t in range(4)] + [("z", g, 0, j) for j in range(2)]
+            rest = [("z", g, 0, j) for j in range(2, 4)] + [("z", g, 1, j) for j in range(4)]
+            if pr == 2:
+                return first + rest
+            return first if pr % 2 == 1 else rest
+
+        def weave(pr, i):
+            todo = woven(pr)
+            n4 = len(todo)
+            for kind, g, q, j in todo[(n4 * i + 3) // 4 : (n4 * (i + 1) + 3) // 4]:
+                if kind == "h":
+                    one_h(g, j)
+                else:
+                    one_z(g, q, j)
+
         def evacuate_h(g, eng_copy):
             hT = front.tile([P, 512], F32, name="hT%d" % g, tag="hT")
             eng_copy(out=hT[:], in_=st[("th", g)][:])
@@ -182,6 +215,8 @@ def tile_treelstm_pb_t_kernel(
                             start=(e == 0),
                             stop=(e == 1 and not pe_bias),
                         )
+                        if kk < 2:
+                            weave(pr, 2 * kk + e)
                     if pe_bias:
                         nc.tensor.matmul(out=dst, lhsT=ones[:], rhs=brow[:, c0:c1], start=False, stop=True)
                 else:
@@ -335,10 +370,6 @@ def tile_treelstm_pb_t_kernel(
             if n < NB:
                 if n not in done_pe:
                     pe_bank(n)
-                pr, k = divmod(n, 6)
-                if k == 5:
-                    if pr % 2 == 1 and (pr + 3) // 2 < NG:
-                        transposes((pr + 3) // 2)
             m = n - LAG
             if m < 0:
                 continue
@@ -346,13 +377,7 @@ def tile_treelstm_pb_t_kernel(
                 v_bank(m)
             pr, k = divmod(m, 6)
             g, q = divmod(pr, 2)
-            if k == 2:
-                if pr - 2 >= VU:
-                    hidden((pr - 2) // 2, nc.vector, 2 * (pr % 2), 2 * (pr % 2) + 2)
-                    store((pr - 2) // 2, 2 * (pr % 2), 2 * (pr % 2) + 2)
-                if pr - 1 >= VU:
-                    cell((pr - 1) // 2, nc.vector, 2 * ((pr - 1) % 2), 2 * ((pr - 1) % 2) + 2)
-                    tanh_c((pr - 1) // 2, 2 * ((pr - 1) % 2), 2 * ((pr - 1) % 2) + 2)
+            pass
             if pr == 1 and k == 4:
                 quantise(1, 0, 2)
             if pr == NPAIR - 1:
@@ -369,8 +394,13 @@ def tile_treelstm_pb_t_kernel(
                 tanh_u(g, 2 * q, 2 * q + 2)
                 if pr + 1 in FLAGGED:
                     s_bank(pr + 1)
+                if q == 0 and 3 <= g + 2 < NG:
+                    evacuate_h(g + 2, nc.scalar.copy)
+                if pr == 1:
+                    evacuate_h(2, nc.scalar.copy)
                 if q == 1 and (pr + 3) // 2 < NG:
-                    evacuate((pr + 3) // 2)
+                    evacuate_z((pr + 3) // 2, 0, nc.scalar.copy)
+                    evacuate_z((pr + 3) // 2, 1, nc.scalar.copy)
                 if q == 0 and 2 <= g + 1 < NG:
                     quantise(g + 1, 0, 2)
                 if q == 1 and pr < VU:
@@ -380,13 +410,18 @@ def tile_treelstm_pb_t_kernel(
                         tanh_c(gg, 0, GT)
                         hidden(gg, nc.gpsimd, 0, GT)
                         store(gg, 0, GT)
-        cell(NG - 1, nc.vector, 2, 3)
-        tanh_c(NG - 1, 2, 3)
-        hidden(NG - 1, nc.vector, 0, 2)
-        store(NG - 1, 0, 2)
-        cell(NG - 1, nc.vector, 3, 4)
-        tanh_c(NG - 1, 3, 4)
-        hidden(NG - 1, nc.vector, 2, 3)
-        store(NG - 1, 2, 3)
-        hidden(NG - 1, nc.vector, 3, 4)
-        store(NG - 1, 3, 4)
+        for pp in range(VU, NPAIR + 2):
+            if pp < NPAIR - 1:
+                cell(pp // 2, nc.vector, 2 * (pp % 2), 2 * (pp % 2) + 2)
+                tanh_c(pp // 2, 2 * (pp % 2), 2 * (pp % 2) + 2)
+            elif pp == NPAIR - 1:
+                for t in (2, 3):
+                    cell(NG - 1, nc.vector, t, t + 1)
+                    tanh_c(NG - 1, t, t + 1)
+            if VU <= pp - 1 < NPAIR - 1:
+                hidden((pp - 1) // 2, nc.vector, 2 * ((pp - 1) % 2), 2 * ((pp - 1) % 2) + 2)
+                store((pp - 1) // 2, 2 * ((pp - 1) % 2), 2 * ((pp - 1) % 2) + 2)
+            elif pp - 1 == NPAIR - 1:
+                for t in (2, 3):
+                    hidden(NG - 1, nc.vector, t, t + 1)
+                    store(NG - 1, t, t + 1)

@@ -21,8 +21,12 @@ NPAIR = 2 * NG
 FLOPS = 2 * B * (SIZE + CH) * 3 * CH
 MANUAL = True
 LAG = 4
-VU = 12
-FLAGGED = (2, 3, 5, 7, 9, 11, 12, 13, 14, 15)
+GH = 2
+GL = 7
+CSPLIT = 5
+FRONT_BUFS = 3
+LOAD_ORDER = (("z", 1), ("h", 1), ("z", 2), ("h", 2), ("f", 0), ("z", 3), ("h", 3), ("f", 1), ("z", 4), ("h", 4), ("f", 2), ("z", 5), ("h", 5), ("f", 3), ("z", 6), ("h", 6), ("f", 4), ("z", 7), ("h", 7), ("f", 5), ("f", 6), ("f", 7))
+FLAGGED = (2, 3, 5, 6, 7, 9, 10, 11, 12, 13, 14, 15)
 
 
 def tile_treelstm_pb_t_kernel(
@@ -33,7 +37,7 @@ def tile_treelstm_pb_t_kernel(
         if MANUAL:
             ctx.enter_context(tc.manual_schedule())
         const = ctx.enter_context(tc.tile_pool(name="const", bufs=1))
-        front = ctx.enter_context(tc.tile_pool(name="front", bufs=2))
+        front = ctx.enter_context(tc.tile_pool(name="front", bufs=FRONT_BUFS))
         pio_pool = ctx.enter_context(tc.tile_pool(name="pio", bufs=5))
         pu_pool = ctx.enter_context(tc.tile_pool(name="pu", bufs=3))
         o_pool = ctx.enter_context(tc.tile_pool(name="osb", bufs=4))
@@ -82,11 +86,8 @@ def tile_treelstm_pb_t_kernel(
         load(z_sb, z0v, 0, 0, 2)
         load_w(w_sb[2], W_u)
         load(z_sb, z0v, 0, 2, 4)
-        load(f_sb, fv, 0)
-        for g in range(1, NG):
-            load(z_sb, z0v, g)
-            load(h_sb, hv, g)
-            load(f_sb, fv, g)
+        for kind, g in LOAD_ORDER:
+            load({"z": z_sb, "h": h_sb, "f": f_sb}[kind], {"z": z0v, "h": hv, "f": fv}[kind], g)
 
         st = {}
 
@@ -123,14 +124,12 @@ def tile_treelstm_pb_t_kernel(
             )
 
         def woven(pr):
-            g = (pr + 3) // 2
+            g = pr // 2 + 2
             if pr < 2 or g >= NG:
                 return []
-            first = [("h", g, 0, t) for t in range(4)] + [("z", g, 0, j) for j in range(2)]
-            rest = [("z", g, 0, j) for j in range(2, 4)] + [("z", g, 1, j) for j in range(4)]
-            if pr == 2:
-                return first + rest
-            return first if pr % 2 == 1 else rest
+            if pr % 2 == 0:
+                return [("z", g, 0, j) for j in range(4)]
+            return [("z", g, 1, j) for j in range(4)] + [("h", g, 0, t) for t in range(4)]
 
         def weave(pr, i):
             todo = woven(pr)
@@ -331,7 +330,7 @@ def tile_treelstm_pb_t_kernel(
             )
         nc.scalar.copy(out=bias[:, 0:512], in_=pb0[:])
         nc.vector.tensor_copy(out=bias[:, 512:1024], in_=pb1[:])
-        HEAD = (("pe", 0), ("v", 0), ("tw", 0), ("ew", 0, "s"), ("pe", 1), ("v", 1), ("tw", 1), ("ew", 1, "s"), ("tz", 0), ("ez", 0, "s"), ("pe", 2), ("v", 2), ("qw", 0), ("tw", 2), ("ew", 2, "s"), ("qz", 0), ("pe", 6), ("v", 6), ("qw", 1), ("tz", 1), ("ez", 1, "s"), ("pe", 7), ("v", 7), ("qz", 1), ("pe", 8), ("v", 8), ("T", 1), ("E", 1))
+        HEAD = (("pe", 0), ("v", 0), ("tw", 0), ("ew", 0, "s"), ("pe", 1), ("v", 1), ("tw", 1), ("ew", 1, "s"), ("tz", 0), ("ez", 0, "s"), ("pe", 2), ("v", 2), ("qw", 0), ("tw", 2), ("ew", 2, "s"), ("qz", 0), ("pe", 6), ("v", 6), ("qw", 1), ("tz", 1), ("ez", 1, "s"), ("pe", 7), ("v", 7), ("qz", 1), ("pe", 8), ("v", 8), ("th", 1), ("eh", 1, "s"), ("tzg", 1, 0), ("ezg", 1, 0, "s"), ("tzg", 1, 1), ("ezg", 1, 1, "s"), ("pe", 3), ("pe", 4), ("pe", 5), ("v", 3), ("v", 4), ("v", 5), ("qg", 1), ("tzg", 2, 0), ("ezg", 2, 0, "s"), ("tzg", 2, 1), ("ezg", 2, 1, "s"), ("th", 2), ("eh", 2, "s"))
         for step in HEAD:
             if step[0] == "tw":
                 transposes_w(step[1])
@@ -354,10 +353,22 @@ def tile_treelstm_pb_t_kernel(
                 evacuate_z(0, step[1], nc.scalar.copy if step[2] == "s" else nc.vector.tensor_copy)
             elif step[0] == "qz":
                 quantise(0, step[1], step[1] + 1)
-            elif step[0] == "T":
-                transposes(step[1])
-            elif step[0] == "E":
-                evacuate(step[1])
+            elif step[0] == "th":
+                transposes_h(step[1])
+            elif step[0] == "eh":
+                evacuate_h(step[1], nc.scalar.copy if step[2] == "s" else nc.vector.tensor_copy)
+            elif step[0] == "tzg":
+                transposes_z(step[1], step[2])
+            elif step[0] == "ezg":
+                evacuate_z(step[1], step[2], nc.scalar.copy if step[3] == "s" else nc.vector.tensor_copy)
+            elif step[0] == "qg":
+                quantise(step[1], 0, 2)
+            elif step[0] == "sig":
+                sig(step[1] // 2, 2 * (step[1] % 2), 2 * (step[1] % 2) + 2)
+            elif step[0] == "tanh":
+                tanh_u(step[1] // 2, 2 * (step[1] % 2), 2 * (step[1] % 2) + 2)
+            elif step[0] == "sb":
+                s_bank(step[1])
             elif step[0] == "pe":
                 pe_bank(step[1])
             elif step[0] == "v":
@@ -366,6 +377,8 @@ def tile_treelstm_pb_t_kernel(
         NB = 6 * NPAIR
         done_pe = set(s[1] for s in HEAD if s[0] == "pe")
         done_v = set(s[1] for s in HEAD if s[0] == "v")
+        done_s = set(s[1] for s in HEAD if s[0] == "tanh")
+        done_sb = set(s[1] for s in HEAD if s[0] == "sb")
         for n in range(NB + LAG):
             if n < NB:
                 if n not in done_pe:
@@ -378,8 +391,6 @@ def tile_treelstm_pb_t_kernel(
             pr, k = divmod(m, 6)
             g, q = divmod(pr, 2)
             pass
-            if pr == 1 and k == 4:
-                quantise(1, 0, 2)
             if pr == NPAIR - 1:
                 if k == 3:
                     sig(g, 2, 3)
@@ -388,40 +399,48 @@ def tile_treelstm_pb_t_kernel(
                 if k == 5:
                     sig(g, 3, 4)
                 continue
-            if k == 4:
+            if k == 4 and pr not in done_s:
                 sig(g, 2 * q, 2 * q + 2)
             if k == 5:
-                tanh_u(g, 2 * q, 2 * q + 2)
-                if pr + 1 in FLAGGED:
+                if pr not in done_s:
+                    tanh_u(g, 2 * q, 2 * q + 2)
+                if pr + 1 in FLAGGED and pr + 1 not in done_sb:
                     s_bank(pr + 1)
-                if q == 0 and 3 <= g + 2 < NG:
-                    evacuate_h(g + 2, nc.scalar.copy)
-                if pr == 1:
-                    evacuate_h(2, nc.scalar.copy)
-                if q == 1 and (pr + 3) // 2 < NG:
-                    evacuate_z((pr + 3) // 2, 0, nc.scalar.copy)
-                    evacuate_z((pr + 3) // 2, 1, nc.scalar.copy)
-                if q == 0 and 2 <= g + 1 < NG:
-                    quantise(g + 1, 0, 2)
-                if q == 1 and pr < VU:
-                    cell(g, nc.gpsimd, 0, GT)
-                for gg in range(VU // 2):
-                    if pr == min(2 * gg + 4, VU + 1):
-                        tanh_c(gg, 0, GT)
-                        hidden(gg, nc.gpsimd, 0, GT)
-                        store(gg, 0, GT)
-        for pp in range(VU, NPAIR + 2):
-            if pp < NPAIR - 1:
-                cell(pp // 2, nc.vector, 2 * (pp % 2), 2 * (pp % 2) + 2)
-                tanh_c(pp // 2, 2 * (pp % 2), 2 * (pp % 2) + 2)
-            elif pp == NPAIR - 1:
-                for t in (2, 3):
-                    cell(NG - 1, nc.vector, t, t + 1)
-                    tanh_c(NG - 1, t, t + 1)
-            if VU <= pp - 1 < NPAIR - 1:
-                hidden((pp - 1) // 2, nc.vector, 2 * ((pp - 1) % 2), 2 * ((pp - 1) % 2) + 2)
-                store((pp - 1) // 2, 2 * ((pp - 1) % 2), 2 * ((pp - 1) % 2) + 2)
-            elif pp - 1 == NPAIR - 1:
-                for t in (2, 3):
-                    hidden(NG - 1, nc.vector, t, t + 1)
-                    store(NG - 1, t, t + 1)
+                if pr >= 2 and g + 2 < NG:
+                    if q == 0:
+                        evacuate_z(g + 2, 0, nc.scalar.copy)
+                        evacuate_z(g + 2, 1, nc.scalar.copy)
+                    else:
+                        evacuate_h(g + 2, nc.scalar.copy)
+                if q == 1:
+                    if g < GL:
+                        cell(g, nc.gpsimd, 0, GT)
+                        if g >= CSPLIT:
+                            store(g, 0, GT, 256, 512)
+                    if 0 <= g - 1 < GL:
+                        tanh_c(g - 1, 0, GT)
+                        if g < GL:
+                            hidden(g - 1, nc.gpsimd, 0, GH)
+                    if g + 2 < NG:
+                        quantise(g + 2, 0, 2)
+                    if g - 2 >= 0:
+                        hidden(g - 2, nc.vector, GH if g - 1 < GL else 0, GT)
+                        if g - 2 >= CSPLIT:
+                            store(g - 2, 0, GT, 0, 256)
+                        else:
+                            store(g - 2, 0, GT)
+        hidden(NG - 3, nc.vector, GH, GT)
+        store(NG - 3, 0, GT, 0, 256)
+        cell(NG - 1, nc.vector, 0, 2)
+        tanh_c(NG - 1, 0, 2)
+        for t in (2, 3):
+            cell(NG - 1, nc.vector, t, t + 1)
+            tanh_c(NG - 1, t, t + 1)
+        tanh_c(NG - 2, 0, GT)
+        hidden(NG - 1, nc.vector, 0, 2)
+        store(NG - 1, 0, 2)
+        for t in (2, 3):
+            hidden(NG - 1, nc.vector, t, t + 1)
+            store(NG - 1, t, t + 1)
+        hidden(NG - 2, nc.vector, 0, GT)
+        store(NG - 2, 0, GT, 0, 256)

@@ -13,20 +13,18 @@ ACT = mybir.ActivationFunctionType
 ALU = mybir.AluOpType
 
 P = 128
-B, SIZE, CH = 4096, 512, 256
-SLOTS = B // P
-GT = 4
-NG = SLOTS // GT
-NPAIR = 2 * NG
-FLOPS = 2 * B * (SIZE + CH) * 3 * CH
-MANUAL = True
-LAG = 4
-GH = 2
-GL = 7
-CSPLIT = 5
-FRONT_BUFS = 3
-LOAD_ORDER = (("z", 1), ("h", 1), ("z", 2), ("h", 2), ("f", 0), ("z", 3), ("h", 3), ("f", 1), ("z", 4), ("h", 4), ("f", 2), ("z", 5), ("h", 5), ("f", 3), ("z", 6), ("h", 6), ("f", 4), ("z", 7), ("h", 7), ("f", 5), ("f", 6), ("f", 7))
-FLAGGED = (2, 3, 5, 6, 7, 9, 10, 11, 12, 13, 14, 15)
+NODES, SIZE, CH = 4096, 512, 256
+TILES = NODES // P
+GROUP = 4
+GROUPS = TILES // GROUP
+PAIRS = TILES // 2
+BANK = 512
+BANKS = 6 * PAIRS
+RING = 5
+LEAD = RING - 1
+FIRST_TENSOR_BIAS = 2
+GPSIMD_H = 2
+FLOPS = 2 * NODES * (SIZE + CH) * 3 * CH
 
 
 def tile_treelstm_pb_t_kernel(
@@ -34,413 +32,342 @@ def tile_treelstm_pb_t_kernel(
 ):
     nc = tc.nc
     with ExitStack() as ctx:
-        if MANUAL:
-            ctx.enter_context(tc.manual_schedule())
-        const = ctx.enter_context(tc.tile_pool(name="const", bufs=1))
-        front = ctx.enter_context(tc.tile_pool(name="front", bufs=FRONT_BUFS))
-        pio_pool = ctx.enter_context(tc.tile_pool(name="pio", bufs=5))
-        pu_pool = ctx.enter_context(tc.tile_pool(name="pu", bufs=3))
-        o_pool = ctx.enter_context(tc.tile_pool(name="osb", bufs=4))
-        tc_pool = ctx.enter_context(tc.tile_pool(name="tcn", bufs=3))
-        ps_t = ctx.enter_context(tc.psum_pool(name="pst", bufs=3))
-        ps_r = ctx.enter_context(tc.psum_pool(name="psr", bufs=5))
+        ctx.enter_context(tc.manual_schedule())
+        keep = ctx.enter_context(tc.tile_pool(name="keep", bufs=1))
+        front = ctx.enter_context(tc.tile_pool(name="front", bufs=3))
+        io_pool = ctx.enter_context(tc.tile_pool(name="io", bufs=4))
+        u_pool = ctx.enter_context(tc.tile_pool(name="u", bufs=3))
+        res_pool = ctx.enter_context(tc.tile_pool(name="res", bufs=4))
+        tanh_pool = ctx.enter_context(tc.tile_pool(name="tanh", bufs=3))
+        turn_psum = ctx.enter_context(tc.psum_pool(name="turn", bufs=8 - RING))
+        sum_psum = ctx.enter_context(tc.psum_pool(name="sums", bufs=RING))
 
-        z0v = z0.rearrange("(p t) k -> p t k", t=SLOTS)
-        hv = h_tilde.rearrange("(p t) k -> p t k", t=SLOTS)
-        fv = fc_sum.rearrange("(p t) k -> p t k", t=SLOTS)
-        ov = out.rearrange("(p t) c -> p t c", t=SLOTS)
+        z_dram = z0.rearrange("(p t) k -> p t k", t=TILES)
+        h_dram = h_tilde.rearrange("(p t) k -> p t k", t=TILES)
+        fc_dram = fc_sum.rearrange("(p t) k -> p t k", t=TILES)
+        out_dram = out.rearrange("(p t) c -> p t c", t=TILES)
 
-        brow = const.tile([P, 768], BF16, name="brow")
-        nc.vector.memset(brow[:].bitcast(I32), 0)
+        bias_rows = keep.tile([P, 3 * CH], BF16, name="bias_rows")
+        nc.vector.memset(bias_rows[:].bitcast(I32), 0)
         for j, b in enumerate((b_i, b_o, b_u)):
             nc.scalar.dma_start(
-                out=brow[0:1, 256 * j : 256 * (j + 1)],
-                in_=b.rearrange("(o n) -> o n", o=1),
+                out=bias_rows[0:1, CH * j : CH * (j + 1)], in_=b.rearrange("(o n) -> o n", o=1)
             )
-        ident = const.tile([P, P], F32, name="ident")
-        make_identity(nc, ident[:])
-        ones = const.tile([P, P], BF16, name="ones")
+        identity = keep.tile([P, P], F32, name="identity")
+        make_identity(nc, identity[:])
+        ones = keep.tile([P, P], BF16, name="ones")
         nc.vector.memset(ones[:], 1.0)
-        warm = const.tile([P, 8], F32, name="warm")
+        warm = keep.tile([P, 8], F32, name="warm")
         nc.vector.memset(warm[:], 0.0)
         nc.scalar.activation(out=warm[:], in_=warm[:], func=ACT.Sigmoid)
 
-        z_sb = [const.tile([P, GT, SIZE], BF16, name="z%d" % g) for g in range(NG)]
-        h_sb = [const.tile([P, GT, CH], BF16, name="h%d" % g) for g in range(NG)]
-        f_sb = [const.tile([P, GT, CH], BF16, name="f%d" % g) for g in range(NG)]
-        w_sb = [const.tile([P, 2, SIZE], BF16, name="w%d" % j) for j in range(3)]
-        u_sb = [const.tile([P, 2, CH], BF16, name="u%d" % j) for j in range(3)]
+        z_in = [keep.tile([P, GROUP, SIZE], BF16, name="z_in%d" % g) for g in range(GROUPS)]
+        h_in = [keep.tile([P, GROUP, CH], BF16, name="h_in%d" % g) for g in range(GROUPS)]
+        fc_in = [keep.tile([P, GROUP, CH], BF16, name="fc_in%d" % g) for g in range(GROUPS)]
+        w_in = [keep.tile([P, 2, SIZE], BF16, name="w_in%d" % j) for j in range(3)]
+        u_in = [keep.tile([P, 2, CH], BF16, name="u_in%d" % j) for j in range(3)]
 
-        def load(dst, src, g, t0=0, t1=GT):
-            nc.sync.dma_start(out=dst[g][:, t0:t1, :], in_=src[:, GT * g + t0 : GT * g + t1, :])
+        def load(dst, src, g, t0=0, t1=GROUP):
+            nc.sync.dma_start(out=dst[g][:, t0:t1, :], in_=src[:, GROUP * g + t0 : GROUP * g + t1, :])
 
-        def load_w(dst, src):
+        def load_weight(dst, src):
             nc.sync.dma_start(out=dst[:], in_=src.rearrange("(b p) k -> p b k", p=P))
 
-        load_w(u_sb[0], U_i)
-        load_w(u_sb[1], U_o)
-        load(h_sb, hv, 0)
-        load_w(u_sb[2], U_u)
-        load_w(w_sb[0], W_i)
-        load_w(w_sb[1], W_o)
-        load(z_sb, z0v, 0, 0, 2)
-        load_w(w_sb[2], W_u)
-        load(z_sb, z0v, 0, 2, 4)
-        for kind, g in LOAD_ORDER:
-            load({"z": z_sb, "h": h_sb, "f": f_sb}[kind], {"z": z0v, "h": hv, "f": fv}[kind], g)
+        load_weight(u_in[0], U_i)
+        load_weight(u_in[1], U_o)
+        load(h_in, h_dram, 0)
+        load_weight(u_in[2], U_u)
+        load_weight(w_in[0], W_i)
+        load_weight(w_in[1], W_o)
+        load(z_in, z_dram, 0, 0, 2)
+        load_weight(w_in[2], W_u)
+        load(z_in, z_dram, 0, 2, 4)
+        for g in range(1, GROUPS):
+            load(z_in, z_dram, g)
+            load(h_in, h_dram, g)
+            if g >= 2:
+                load(fc_in, fc_dram, g - 2)
+        load(fc_in, fc_dram, GROUPS - 2)
+        load(fc_in, fc_dram, GROUPS - 1)
 
-        st = {}
+        def words(tile_ap):
+            return tile_ap[:].rearrange("p a k -> p (a k)").bitcast(F32)
 
-        def transposes_h(g):
-            hf = h_sb[g][:].rearrange("p t k -> p (t k)").bitcast(F32)
-            th = ps_t.tile([P, 512], F32, name="th%d" % g, tag="T")
-            for t in range(GT):
-                nc.tensor.transpose(th[:, P * t : P * (t + 1)], hf[:, P * t : P * (t + 1)], ident[:])
-            st[("th", g)] = th
-
-        def transposes_z(g, q):
-            zf = z_sb[g][:].rearrange("p t k -> p (t k)").bitcast(F32)
-            tzq = ps_t.tile([P, 512], F32, name="tz%d_%d" % (g, q), tag="T")
-            for s in range(2):
-                for u in range(2):
-                    c = 256 * (2 * q + s) + P * u
-                    nc.tensor.transpose(
-                        tzq[:, 256 * s + P * u : 256 * s + P * (u + 1)], zf[:, c : c + P], ident[:]
-                    )
-            st[("tz", g, q)] = tzq
-
-        def one_h(g, t):
-            if t == 0:
-                st[("th", g)] = ps_t.tile([P, 512], F32, name="th%d" % g, tag="T")
-            hf = h_sb[g][:].rearrange("p t k -> p (t k)").bitcast(F32)
-            nc.tensor.transpose(st[("th", g)][:, P * t : P * (t + 1)], hf[:, P * t : P * (t + 1)], ident[:])
-
-        def one_z(g, q, j):
-            if j == 0:
-                st[("tz", g, q)] = ps_t.tile([P, 512], F32, name="tz%d_%d" % (g, q), tag="T")
-            zf = z_sb[g][:].rearrange("p t k -> p (t k)").bitcast(F32)
+        def turn(bank, at, src_words, block):
             nc.tensor.transpose(
-                st[("tz", g, q)][:, P * j : P * (j + 1)], zf[:, 512 * q + P * j : 512 * q + P * (j + 1)], ident[:]
+                bank[:, P * at : P * (at + 1)], src_words[:, P * block : P * (block + 1)], identity[:]
             )
 
-        def woven(pr):
-            g = pr // 2 + 2
-            if pr < 2 or g >= NG:
-                return []
-            if pr % 2 == 0:
-                return [("z", g, 0, j) for j in range(4)]
-            return [("z", g, 1, j) for j in range(4)] + [("h", g, 0, t) for t in range(4)]
+        h_bank, z_bank = {}, {}
 
-        def weave(pr, i):
-            todo = woven(pr)
-            n4 = len(todo)
-            for kind, g, q, j in todo[(n4 * i + 3) // 4 : (n4 * (i + 1) + 3) // 4]:
-                if kind == "h":
-                    one_h(g, j)
-                else:
-                    one_z(g, q, j)
+        def turn_h(g, j):
+            if j == 0:
+                h_bank[g] = turn_psum.tile([P, BANK], F32, name="h_bank%d" % g, tag="turn")
+            turn(h_bank[g], j, words(h_in[g]), j)
 
-        def evacuate_h(g, eng_copy):
-            hT = front.tile([P, 512], F32, name="hT%d" % g, tag="hT")
-            eng_copy(out=hT[:], in_=st[("th", g)][:])
-            st[("hT", g)] = hT
+        def turn_z(g, half, j):
+            if j == 0:
+                z_bank[g, half] = turn_psum.tile([P, BANK], F32, name="z_bank%d_%d" % (g, half), tag="turn")
+            turn(z_bank[g, half], j, words(z_in[g]), 4 * half + j)
 
-        def regroup(eng_copy, dst_f32, bank):
-            eng_copy(
-                out=dst_f32.rearrange("p (s m u) -> p s m u", s=2, m=P, u=2),
-                in_=bank[:].rearrange("p (s u m) -> p s m u", s=2, u=2, m=P),
+        def regroup(copy, dst_words, bank):
+            copy(
+                out=dst_words.rearrange("p (s m v) -> p s m v", s=2, m=P, v=2),
+                in_=bank[:].rearrange("p (s v m) -> p s m v", s=2, v=2, m=P),
             )
 
-        def evacuate_z(g, q, eng_copy):
-            if q == 0:
-                st[("gz", g)] = front.tile([P, 2048], BF16, name="gz%d" % g, tag="gz", align_bytes=64)
-            gzf = st[("gz", g)][:].bitcast(F32)
-            regroup(eng_copy, gzf[:, 512 * q : 512 * (q + 1)], st[("tz", g, q)])
+        hT, z_grouped, z_codes, z_scales = {}, {}, {}, {}
 
-        def quantise(g, q0, q1):
-            gz = st[("gz", g)]
-            if q0 == 0:
-                zc = front.tile([P, 512], U32, name="zc%d" % g, tag="zc", align_bytes=64)
-                zs = front.tile([P, 512], U8, name="zs%d" % g, tag="zs", align_bytes=64)
-                st[("zc", g)] = (zc, zs)
-            zc, zs = st[("zc", g)]
+        def copy_h(g):
+            hT[g] = front.tile([P, BANK], F32, name="hT%d" % g, tag="hT")
+            nc.scalar.copy(out=hT[g][:], in_=h_bank[g][:])
+
+        def regroup_z(g, half):
+            if half == 0:
+                z_grouped[g] = front.tile([P, 4 * BANK], BF16, name="z_grouped%d" % g, tag="zg", align_bytes=64)
+            regroup(nc.scalar.copy, z_grouped[g][:].bitcast(F32)[:, BANK * half : BANK * (half + 1)], z_bank[g, half])
+
+        def quantise_z(g, half0=0, half1=2):
+            if half0 == 0:
+                z_codes[g] = front.tile([P, BANK], U32, name="z_codes%d" % g, tag="zc", align_bytes=64)
+                z_scales[g] = front.tile([P, BANK], U8, name="z_scales%d" % g, tag="zs", align_bytes=64)
             nc.vector.quantize_mx(
-                out=zc[:, 256 * q0 : 256 * q1].bitcast(FP8X4),
-                scales=zs[:, 256 * q0 : 256 * q1],
-                in_=gz[:, 1024 * q0 : 1024 * q1],
+                out=z_codes[g][:, 2 * P * half0 : 2 * P * half1].bitcast(FP8X4),
+                scales=z_scales[g][:, 2 * P * half0 : 2 * P * half1],
+                in_=z_grouped[g][:, 8 * P * half0 : 8 * P * half1],
             )
 
-        def transposes(g):
-            transposes_h(g)
-            transposes_z(g, 0)
-            transposes_z(g, 1)
+        def front_h(g):
+            for j in range(GROUP):
+                turn_h(g, j)
+            copy_h(g)
 
-        def evacuate(g):
-            evacuate_h(g, nc.scalar.copy)
-            evacuate_z(g, 0, nc.scalar.copy)
-            evacuate_z(g, 1, nc.scalar.copy)
+        def front_z(g, half):
+            for j in range(4):
+                turn_z(g, half, j)
+            regroup_z(g, half)
 
-        UTw = const.tile([P, 768], F32, name="UTw")
-        UT = UTw[:].bitcast(BF16).rearrange("p (n e) -> p n e", e=2)
-        bias = const.tile([P, 1024], F32, name="bias")
-        gw = const.tile([P, 3072], BF16, name="gw", align_bytes=64)
-        gwf = gw[:].bitcast(F32)
-        wc = const.tile([P, 768], U32, name="wc", align_bytes=64)
-        ws = const.tile([P, 768], U8, name="ws", align_bytes=64)
+        def ride(pair, j):
+            g = pair // 2 + 2
+            if 3 <= g < GROUPS:
+                turn_z(g, pair % 2, j)
+                if pair % 2 == 1:
+                    turn_h(g, j)
 
-        def kk_of(pr, k):
-            return (0, 2, 1)[k % 3] if pr == NPAIR - 1 else k % 3
+        uT_words = keep.tile([P, 3 * CH], F32, name="uT_words")
+        uT = uT_words[:].bitcast(BF16).rearrange("p (n e) -> p n e", e=2)
+        bias_all = keep.tile([P, 2 * BANK], F32, name="bias_all")
+        w_grouped = keep.tile([P, 12 * CH], BF16, name="w_grouped", align_bytes=64)
+        w_codes = keep.tile([P, 3 * CH], U32, name="w_codes", align_bytes=64)
+        w_scales = keep.tile([P, 3 * CH], U8, name="w_scales", align_bytes=64)
 
-        def pe_bank(n):
-            pr, k = divmod(n, 6)
-            g, q = divmod(pr, 2)
-            r = ps_r.tile([P, 512], F32, name="r%d" % n, tag="R")
-            st[("r", n)] = r
-            kk = kk_of(pr, k)
-            if kk < 2:
-                parts = [(2 * q + kk, 0, 512, 0)]
+        def front_w(j):
+            bank = sum_psum.tile([P, BANK], F32, name="w_bank%d" % j, tag="sum")
+            for block in range(4):
+                turn(bank, block, words(w_in[j]), block)
+            regroup(nc.scalar.copy, w_grouped[:].bitcast(F32)[:, BANK * j : BANK * (j + 1)], bank)
+
+        def quantise_w(c0, c1):
+            nc.vector.quantize_mx(
+                out=w_codes[:, c0:c1].bitcast(FP8X4), scales=w_scales[:, c0:c1], in_=w_grouped[:, 4 * c0 : 4 * c1]
+            )
+
+        sums, gates_io, gates_u = {}, {}, {}
+
+        def tensor_bias(pair):
+            return pair >= FIRST_TENSOR_BIAS
+
+        def tensor_bank(n):
+            pair, k = divmod(n, 6)
+            g, second = divmod(pair, 2)
+            sums[n] = sum_psum.tile([P, BANK], F32, name="sums%d" % n, tag="sum")
+            if k % 3 < 2:
+                parts = [(2 * second + k % 3, 0, BANK, 0)]
             else:
-                parts = [(2 * q, 512, 768, 0), (2 * q + 1, 512, 768, 256)]
-            for t, c0, c1, o0 in parts:
-                dst = r[:, o0 : o0 + (c1 - c0)]
-                if k < 3:
-                    hT = st[("hT", g)][:].bitcast(BF16).rearrange("p (t m e) -> p t m e", t=GT, m=P, e=2)
-                    pe_bias = kk == 2 and pr in FLAGGED
-                    for e in range(2):
-                        nc.tensor.matmul(
-                            out=dst,
-                            lhsT=hT[:, t, :, e],
-                            rhs=UT[:, c0:c1, e],
-                            start=(e == 0),
-                            stop=(e == 1 and not pe_bias),
-                        )
-                        if kk < 2:
-                            weave(pr, 2 * kk + e)
-                    if pe_bias:
-                        nc.tensor.matmul(out=dst, lhsT=ones[:], rhs=brow[:, c0:c1], start=False, stop=True)
-                else:
-                    zc, zs = st[("zc", g)]
+                parts = [(2 * second, BANK, 3 * CH, 0), (2 * second + 1, BANK, 3 * CH, CH)]
+            for t, c0, c1, at in parts:
+                dst = sums[n][:, at : at + c1 - c0]
+                if k >= 3:
                     nc.tensor.matmul_mx(
                         out=dst,
-                        lhsT=zc[:, P * t : P * (t + 1)].bitcast(FP8X4),
-                        lhsT_scale=zs[:, P * t : P * (t + 1)],
-                        rhs=wc[:, c0:c1].bitcast(FP8X4),
-                        rhs_scale=ws[:, c0:c1],
+                        lhsT=z_codes[g][:, P * t : P * (t + 1)].bitcast(FP8X4),
+                        lhsT_scale=z_scales[g][:, P * t : P * (t + 1)],
+                        rhs=w_codes[:, c0:c1].bitcast(FP8X4),
+                        rhs_scale=w_scales[:, c0:c1],
                         start=True,
                         stop=True,
                     )
+                    continue
+                h_tile = hT[g][:].bitcast(BF16).rearrange("p (t m e) -> p t m e", t=GROUP, m=P, e=2)
+                with_bias = k == 2 and tensor_bias(pair)
+                for e in range(2):
+                    nc.tensor.matmul(
+                        out=dst,
+                        lhsT=h_tile[:, t, :, e],
+                        rhs=uT[:, c0:c1, e],
+                        start=(e == 0),
+                        stop=(e == 1 and not with_bias),
+                    )
+                    if k < 2:
+                        ride(pair, 2 * k + e)
+                if with_bias:
+                    nc.tensor.matmul(out=dst, lhsT=ones[:], rhs=bias_rows[:, c0:c1], start=False, stop=True)
 
-        def pre_slice(g, q, kk):
-            if kk < 2:
-                return st[("pio", g)][:, 512 * (2 * q + kk) : 512 * (2 * q + kk + 1)]
-            return st[("pu", g)][:, 512 * q : 512 * (q + 1)]
+        def gate_slice(pair, k):
+            g, second = divmod(pair, 2)
+            if g not in gates_io:
+                gates_io[g] = io_pool.tile([P, GROUP * BANK], F32, name="gates_io%d" % g, tag="io")
+                gates_u[g] = u_pool.tile([P, GROUP * CH], F32, name="gates_u%d" % g, tag="u")
+            if k % 3 < 2:
+                t = 2 * second + k % 3
+                return gates_io[g][:, BANK * t : BANK * (t + 1)]
+            return gates_u[g][:, BANK * second : BANK * (second + 1)]
 
-        def alloc_pre(g):
-            if ("pio", g) not in st:
-                st[("pio", g)] = pio_pool.tile([P, 2048], F32, name="pio%d" % g, tag="pio")
-                st[("pu", g)] = pu_pool.tile([P, 1024], F32, name="pu%d" % g, tag="pu")
-
-        def v_bank(n):
-            pr, k = divmod(n, 6)
-            g, q = divmod(pr, 2)
-            alloc_pre(g)
-            kk = kk_of(pr, k)
-            if k < 3 and kk == 2 and pr in FLAGGED:
+        def vector_bank(n):
+            pair, k = divmod(n, 6)
+            if k == 2 and tensor_bias(pair):
                 return
-            dst = pre_slice(g, q, kk)
-            other = dst if k >= 3 else (bias[:, 0:512] if kk < 2 else bias[:, 512:1024])
-            nc.vector.tensor_tensor(out=dst, in0=st[("r", n)][:], in1=other, op=ALU.add)
+            dst = gate_slice(pair, k)
+            if k >= 3:
+                other = dst
+            else:
+                other = bias_all[:, 0:BANK] if k < 2 else bias_all[:, BANK : 2 * BANK]
+            nc.vector.tensor_tensor(out=dst, in0=sums[n][:], in1=other, op=ALU.add)
 
-        def s_bank(pr):
-            g, q = divmod(pr, 2)
-            alloc_pre(g)
-            nc.scalar.copy(out=pre_slice(g, q, 2), in_=st[("r", 6 * pr + (1 if pr == NPAIR - 1 else 2))][:])
+        def scalar_bank(pair):
+            nc.scalar.copy(out=gate_slice(pair, 2), in_=sums[6 * pair + 2][:])
 
-        def sig(g, t0, t1):
-            v = st[("pio", g)][:, 512 * t0 : 512 * t1]
+        def sigmoid_io(pair):
+            g, second = divmod(pair, 2)
+            v = gates_io[g][:, 2 * BANK * second : 2 * BANK * (second + 1)]
             nc.scalar.activation(out=v, in_=v, func=ACT.Sigmoid)
 
-        def tanh_u(g, t0, t1):
-            v = st[("pu", g)][:, 256 * t0 : 256 * t1]
+        def tanh_u(pair):
+            v = gate_slice(pair, 2)
             nc.scalar.activation(out=v, in_=v, func=ACT.Tanh)
 
-        def views(g, t0, t1):
-            io = st[("pio", g)][:].rearrange("p (t c) -> p t c", c=512)
-            uu = st[("pu", g)][:].rearrange("p (t c) -> p t c", c=256)
-            oo = st[("o", g)][:]
-            return (
-                io[:, t0:t1, 0:256],
-                io[:, t0:t1, 256:512],
-                uu[:, t0:t1, :],
-                oo[:, t0:t1, 0:256],
-                oo[:, t0:t1, 256:512],
-            )
+        res, tanh_c_sb = {}, {}
 
-        def cell(g, eng, t0, t1):
-            if ("o", g) not in st:
-                st[("o", g)] = o_pool.tile([P, GT, 512], F32, name="o%d" % g, tag="o")
-            gi, go, gu, oh, oc = views(g, t0, t1)
-            eng.tensor_tensor(out=oc, in0=gi, in1=gu, op=ALU.mult)
-            eng.tensor_tensor(out=oc, in0=oc, in1=f_sb[g][:, t0:t1, :], op=ALU.add)
+        def cell(engine, g, t0, t1):
+            if g not in res:
+                res[g] = res_pool.tile([P, GROUP, 2 * CH], F32, name="res%d" % g, tag="res")
+                tanh_c_sb[g] = tanh_pool.tile([P, GROUP, CH], F32, name="tanh_c%d" % g, tag="tanh")
+            io = gates_io[g][:].rearrange("p (t c) -> p t c", c=BANK)
+            uu = gates_u[g][:].rearrange("p (t c) -> p t c", c=CH)
+            c = res[g][:, t0:t1, CH : 2 * CH]
+            engine.tensor_tensor(out=c, in0=io[:, t0:t1, 0:CH], in1=uu[:, t0:t1, :], op=ALU.mult)
+            engine.tensor_tensor(out=c, in0=c, in1=fc_in[g][:, t0:t1, :], op=ALU.add)
+            store(g, t0, t1, CH, 2 * CH)
 
         def tanh_c(g, t0, t1):
-            if ("tc", g) not in st:
-                st[("tc", g)] = tc_pool.tile([P, GT, 256], F32, name="tc%d" % g, tag="tc")
-            gi, go, gu, oh, oc = views(g, t0, t1)
-            nc.scalar.activation(out=st[("tc", g)][:, t0:t1, :], in_=oc, func=ACT.Tanh)
+            nc.scalar.activation(out=tanh_c_sb[g][:, t0:t1, :], in_=res[g][:, t0:t1, CH : 2 * CH], func=ACT.Tanh)
 
-        def hidden(g, eng, t0, t1):
-            gi, go, gu, oh, oc = views(g, t0, t1)
-            eng.tensor_tensor(out=oh, in0=go, in1=st[("tc", g)][:, t0:t1, :], op=ALU.mult)
-
-        def store(g, t0, t1, c0=0, c1=512):
-            nc.sync.dma_start(
-                out=ov[:, GT * g + t0 : GT * g + t1, c0:c1], in_=st[("o", g)][:, t0:t1, c0:c1]
+        def hidden(engine, g, t0, t1):
+            io = gates_io[g][:].rearrange("p (t c) -> p t c", c=BANK)
+            engine.tensor_tensor(
+                out=res[g][:, t0:t1, 0:CH], in0=io[:, t0:t1, CH:BANK], in1=tanh_c_sb[g][:, t0:t1, :], op=ALU.mult
             )
 
-        tuA = ps_r.tile([P, 512], F32, name="tuA", tag="R")
-        tuB = ps_r.tile([P, 512], F32, name="tuB", tag="R")
+        def store(g, t0, t1, c0, c1):
+            nc.sync.dma_start(out=out_dram[:, GROUP * g + t0 : GROUP * g + t1, c0:c1], in_=res[g][:, t0:t1, c0:c1])
 
-        def transposes_u(j):
-            uf = u_sb[j][:].rearrange("p b k -> p (b k)").bitcast(F32)
+        def after_pair(pair):
+            g, second = divmod(pair, 2)
+            if pair + 1 < PAIRS and tensor_bias(pair + 1):
+                scalar_bank(pair + 1)
+            ahead = g + 2
+            if not second:
+                if 3 <= ahead < GROUPS:
+                    regroup_z(ahead, 0)
+                    regroup_z(ahead, 1)
+                return
+            if 3 <= ahead < GROUPS:
+                copy_h(ahead)
+            if g < GROUPS - 1:
+                cell(nc.gpsimd, g, 0, GROUP)
+            if g >= 1:
+                tanh_c(g - 1, 0, GROUP)
+                if g < GROUPS - 1:
+                    hidden(nc.gpsimd, g - 1, 0, GPSIMD_H)
+            if ahead < GROUPS:
+                quantise_z(ahead)
+            if g >= 2:
+                hidden(nc.vector, g - 2, GPSIMD_H, GROUP)
+                store(g - 2, 0, GROUP, 0, CH)
+
+        u_bank = [sum_psum.tile([P, BANK], F32, name="u_bank%d" % j, tag="sum") for j in range(2)]
+        for j in range(2):
             for b in range(2):
-                dst = tuA[:, 256 * j + P * b : 256 * j + P * (b + 1)] if j < 2 else tuB[:, P * b : P * (b + 1)]
-                nc.tensor.transpose(dst, uf[:, P * b : P * (b + 1)], ident[:])
-
-        def transposes_w(j):
-            wf = w_sb[j][:].rearrange("p b k -> p (b k)").bitcast(F32)
-            tw = ps_r.tile([P, 512], F32, name="tw%d" % j, tag="R")
-            for c in range(4):
-                nc.tensor.transpose(tw[:, P * c : P * (c + 1)], wf[:, P * c : P * (c + 1)], ident[:])
-            st[("tw", j)] = tw
-
-        transposes_u(0)
-        transposes_u(1)
-        nc.vector.tensor_copy(out=UTw[:, 0:512], in_=tuA[:])
-        transposes_h(0)
-        evacuate_h(0, nc.scalar.copy)
-        transposes_u(2)
-        nc.vector.tensor_copy(out=UTw[:, 512:768], in_=tuB[:, 0:256])
-        pb0 = ps_r.tile([P, 512], F32, name="pb0", tag="R")
-        nc.tensor.matmul(out=pb0[:], lhsT=ones[:], rhs=brow[:, 0:512], start=True, stop=True)
-        pb1 = ps_r.tile([P, 512], F32, name="pb1", tag="R")
+                turn(u_bank[0], 2 * j + b, words(u_in[j]), b)
+        nc.vector.tensor_copy(out=uT_words[:, 0:BANK], in_=u_bank[0][:])
+        front_h(0)
+        for b in range(2):
+            turn(u_bank[1], b, words(u_in[2]), b)
+        nc.vector.tensor_copy(out=uT_words[:, BANK : 3 * CH], in_=u_bank[1][:, 0:CH])
+        bias_io = sum_psum.tile([P, BANK], F32, name="bias_io", tag="sum")
+        nc.tensor.matmul(out=bias_io[:], lhsT=ones[:], rhs=bias_rows[:, 0:BANK], start=True, stop=True)
+        bias_uu = sum_psum.tile([P, BANK], F32, name="bias_uu", tag="sum")
         for j in range(2):
             nc.tensor.matmul(
-                out=pb1[:, 256 * j : 256 * (j + 1)], lhsT=ones[:], rhs=brow[:, 512:768], start=True, stop=True
+                out=bias_uu[:, CH * j : CH * (j + 1)], lhsT=ones[:], rhs=bias_rows[:, BANK : 3 * CH], start=True, stop=True
             )
-        nc.scalar.copy(out=bias[:, 0:512], in_=pb0[:])
-        nc.vector.tensor_copy(out=bias[:, 512:1024], in_=pb1[:])
-        HEAD = (("pe", 0), ("v", 0), ("tw", 0), ("ew", 0, "s"), ("pe", 1), ("v", 1), ("tw", 1), ("ew", 1, "s"), ("tz", 0), ("ez", 0, "s"), ("pe", 2), ("v", 2), ("qw", 0), ("tw", 2), ("ew", 2, "s"), ("qz", 0), ("pe", 6), ("v", 6), ("qw", 1), ("tz", 1), ("ez", 1, "s"), ("pe", 7), ("v", 7), ("qz", 1), ("pe", 8), ("v", 8), ("th", 1), ("eh", 1, "s"), ("tzg", 1, 0), ("ezg", 1, 0, "s"), ("tzg", 1, 1), ("ezg", 1, 1, "s"), ("pe", 3), ("pe", 4), ("pe", 5), ("v", 3), ("v", 4), ("v", 5), ("qg", 1), ("tzg", 2, 0), ("ezg", 2, 0, "s"), ("tzg", 2, 1), ("ezg", 2, 1, "s"), ("th", 2), ("eh", 2, "s"))
-        for step in HEAD:
-            if step[0] == "tw":
-                transposes_w(step[1])
-            elif step[0] == "ew":
-                regroup(
-                    nc.scalar.copy if step[2] == "s" else nc.vector.tensor_copy,
-                    gwf[:, 512 * step[1] : 512 * (step[1] + 1)],
-                    st[("tw", step[1])],
-                )
-            elif step[0] == "qw":
-                if step[1] == 0:
-                    nc.vector.quantize_mx(out=wc[:, 0:512].bitcast(FP8X4), scales=ws[:, 0:512], in_=gw[:, 0:2048])
-                else:
-                    nc.vector.quantize_mx(
-                        out=wc[:, 512:768].bitcast(FP8X4), scales=ws[:, 512:768], in_=gw[:, 2048:3072]
-                    )
-            elif step[0] == "tz":
-                transposes_z(0, step[1])
-            elif step[0] == "ez":
-                evacuate_z(0, step[1], nc.scalar.copy if step[2] == "s" else nc.vector.tensor_copy)
-            elif step[0] == "qz":
-                quantise(0, step[1], step[1] + 1)
-            elif step[0] == "th":
-                transposes_h(step[1])
-            elif step[0] == "eh":
-                evacuate_h(step[1], nc.scalar.copy if step[2] == "s" else nc.vector.tensor_copy)
-            elif step[0] == "tzg":
-                transposes_z(step[1], step[2])
-            elif step[0] == "ezg":
-                evacuate_z(step[1], step[2], nc.scalar.copy if step[3] == "s" else nc.vector.tensor_copy)
-            elif step[0] == "qg":
-                quantise(step[1], 0, 2)
-            elif step[0] == "sig":
-                sig(step[1] // 2, 2 * (step[1] % 2), 2 * (step[1] % 2) + 2)
-            elif step[0] == "tanh":
-                tanh_u(step[1] // 2, 2 * (step[1] % 2), 2 * (step[1] % 2) + 2)
-            elif step[0] == "sb":
-                s_bank(step[1])
-            elif step[0] == "pe":
-                pe_bank(step[1])
-            elif step[0] == "v":
-                v_bank(step[1])
+        nc.scalar.copy(out=bias_all[:, 0:BANK], in_=bias_io[:])
+        nc.vector.tensor_copy(out=bias_all[:, BANK : 2 * BANK], in_=bias_uu[:])
 
-        NB = 6 * NPAIR
-        done_pe = set(s[1] for s in HEAD if s[0] == "pe")
-        done_v = set(s[1] for s in HEAD if s[0] == "v")
-        done_s = set(s[1] for s in HEAD if s[0] == "tanh")
-        done_sb = set(s[1] for s in HEAD if s[0] == "sb")
-        for n in range(NB + LAG):
-            if n < NB:
-                if n not in done_pe:
-                    pe_bank(n)
-            m = n - LAG
-            if m < 0:
+        def plain_bank(n):
+            tensor_bank(n)
+            vector_bank(n)
+
+        plain_bank(0)
+        front_w(0)
+        plain_bank(1)
+        front_w(1)
+        front_z(0, 0)
+        plain_bank(2)
+        quantise_w(0, BANK)
+        front_w(2)
+        quantise_z(0, 0, 1)
+        plain_bank(6)
+        quantise_w(BANK, 3 * CH)
+        front_z(0, 1)
+        plain_bank(7)
+        quantise_z(0, 1, 2)
+        plain_bank(8)
+        front_h(1)
+        front_z(1, 0)
+        front_z(1, 1)
+        for n in (3, 4, 5):
+            tensor_bank(n)
+        for n in (3, 4, 5):
+            vector_bank(n)
+        quantise_z(1)
+        front_z(2, 0)
+        front_z(2, 1)
+        front_h(2)
+        sigmoid_io(0)
+        tanh_u(0)
+        after_pair(0)
+
+        done = 9
+        for n in range(done, BANKS + LEAD):
+            if n < BANKS:
+                tensor_bank(n)
+            if n - LEAD < done:
                 continue
-            if m not in done_v:
-                v_bank(m)
-            pr, k = divmod(m, 6)
-            g, q = divmod(pr, 2)
-            pass
-            if pr == NPAIR - 1:
-                if k == 3:
-                    sig(g, 2, 3)
-                if k == 4:
-                    tanh_u(g, 2, 4)
-                if k == 5:
-                    sig(g, 3, 4)
-                continue
-            if k == 4 and pr not in done_s:
-                sig(g, 2 * q, 2 * q + 2)
+            pair, k = divmod(n - LEAD, 6)
+            vector_bank(n - LEAD)
+            if k == 4:
+                sigmoid_io(pair)
             if k == 5:
-                if pr not in done_s:
-                    tanh_u(g, 2 * q, 2 * q + 2)
-                if pr + 1 in FLAGGED and pr + 1 not in done_sb:
-                    s_bank(pr + 1)
-                if pr >= 2 and g + 2 < NG:
-                    if q == 0:
-                        evacuate_z(g + 2, 0, nc.scalar.copy)
-                        evacuate_z(g + 2, 1, nc.scalar.copy)
-                    else:
-                        evacuate_h(g + 2, nc.scalar.copy)
-                if q == 1:
-                    if g < GL:
-                        cell(g, nc.gpsimd, 0, GT)
-                        if g >= CSPLIT:
-                            store(g, 0, GT, 256, 512)
-                    if 0 <= g - 1 < GL:
-                        tanh_c(g - 1, 0, GT)
-                        if g < GL:
-                            hidden(g - 1, nc.gpsimd, 0, GH)
-                    if g + 2 < NG:
-                        quantise(g + 2, 0, 2)
-                    if g - 2 >= 0:
-                        hidden(g - 2, nc.vector, GH if g - 1 < GL else 0, GT)
-                        if g - 2 >= CSPLIT:
-                            store(g - 2, 0, GT, 0, 256)
-                        else:
-                            store(g - 2, 0, GT)
-        hidden(NG - 3, nc.vector, GH, GT)
-        store(NG - 3, 0, GT, 0, 256)
-        cell(NG - 1, nc.vector, 0, 2)
-        tanh_c(NG - 1, 0, 2)
-        for t in (2, 3):
-            cell(NG - 1, nc.vector, t, t + 1)
-            tanh_c(NG - 1, t, t + 1)
-        tanh_c(NG - 2, 0, GT)
-        hidden(NG - 1, nc.vector, 0, 2)
-        store(NG - 1, 0, 2)
-        for t in (2, 3):
-            hidden(NG - 1, nc.vector, t, t + 1)
-            store(NG - 1, t, t + 1)
-        hidden(NG - 2, nc.vector, 0, GT)
-        store(NG - 2, 0, GT, 0, 256)
+                tanh_u(pair)
+                after_pair(pair)
+
+        last = GROUPS - 1
+        for t0 in (0, 2):
+            cell(nc.vector, last, t0, t0 + 2)
+            tanh_c(last, t0, t0 + 2)
+        hidden(nc.vector, last - 1, 0, GROUP)
+        store(last - 1, 0, GROUP, 0, CH)
+        for t0 in (0, 2):
+            hidden(nc.vector, last, t0, t0 + 2)
+            store(last, t0, t0 + 2, 0, CH)

@@ -19,9 +19,11 @@ GROUP = 4
 GROUPS = TILES // GROUP
 PAIRS = TILES // 2
 BANK = 512
-BANKS = 6 * PAIRS
+FILLS = 6 * PAIRS
 RING = 5
 LEAD = RING - 1
+HEAD_GROUPS = 3
+HEAD_FILLS = 9
 FIRST_TENSOR_BIAS = 2
 GPSIMD_H = 2
 FLOPS = 2 * NODES * (SIZE + CH) * 3 * CH
@@ -93,9 +95,9 @@ def tile_treelstm_pb_t_kernel(
         def words(tile_ap):
             return tile_ap[:].rearrange("p a k -> p (a k)").bitcast(F32)
 
-        def turn(bank, at, src_words, block):
+        def turn(bank, at, src_words, square):
             nc.tensor.transpose(
-                bank[:, P * at : P * (at + 1)], src_words[:, P * block : P * (block + 1)], identity[:]
+                bank[:, P * at : P * (at + 1)], src_words[:, P * square : P * (square + 1)], identity[:]
             )
 
         h_bank, z_bank = {}, {}
@@ -110,8 +112,8 @@ def tile_treelstm_pb_t_kernel(
                 z_bank[g, half] = turn_psum.tile([P, BANK], F32, name="z_bank%d_%d" % (g, half), tag="turn")
             turn(z_bank[g, half], j, words(z_in[g]), 4 * half + j)
 
-        def regroup(copy, dst_words, bank):
-            copy(
+        def regroup(dst_words, bank):
+            nc.scalar.copy(
                 out=dst_words.rearrange("p (s m v) -> p s m v", s=2, m=P, v=2),
                 in_=bank[:].rearrange("p (s v m) -> p s m v", s=2, v=2, m=P),
             )
@@ -124,8 +126,10 @@ def tile_treelstm_pb_t_kernel(
 
         def regroup_z(g, half):
             if half == 0:
-                z_grouped[g] = front.tile([P, 4 * BANK], BF16, name="z_grouped%d" % g, tag="zg", align_bytes=64)
-            regroup(nc.scalar.copy, z_grouped[g][:].bitcast(F32)[:, BANK * half : BANK * (half + 1)], z_bank[g, half])
+                z_grouped[g] = front.tile(
+                    [P, 4 * BANK], BF16, name="z_grouped%d" % g, tag="zg", align_bytes=64
+                )
+            regroup(z_grouped[g][:].bitcast(F32)[:, BANK * half : BANK * (half + 1)], z_bank[g, half])
 
         def quantise_z(g, half0=0, half1=2):
             if half0 == 0:
@@ -149,7 +153,7 @@ def tile_treelstm_pb_t_kernel(
 
         def ride(pair, j):
             g = pair // 2 + 2
-            if 3 <= g < GROUPS:
+            if HEAD_GROUPS <= g < GROUPS:
                 turn_z(g, pair % 2, j)
                 if pair % 2 == 1:
                     turn_h(g, j)
@@ -163,9 +167,9 @@ def tile_treelstm_pb_t_kernel(
 
         def front_w(j):
             bank = sum_psum.tile([P, BANK], F32, name="w_bank%d" % j, tag="sum")
-            for block in range(4):
-                turn(bank, block, words(w_in[j]), block)
-            regroup(nc.scalar.copy, w_grouped[:].bitcast(F32)[:, BANK * j : BANK * (j + 1)], bank)
+            for square in range(4):
+                turn(bank, square, words(w_in[j]), square)
+            regroup(w_grouped[:].bitcast(F32)[:, BANK * j : BANK * (j + 1)], bank)
 
         def quantise_w(c0, c1):
             nc.vector.quantize_mx(
@@ -177,7 +181,7 @@ def tile_treelstm_pb_t_kernel(
         def tensor_bias(pair):
             return pair >= FIRST_TENSOR_BIAS
 
-        def tensor_bank(n):
+        def tensor_fill(n):
             pair, k = divmod(n, 6)
             g, second = divmod(pair, 2)
             sums[n] = sum_psum.tile([P, BANK], F32, name="sums%d" % n, tag="sum")
@@ -223,7 +227,7 @@ def tile_treelstm_pb_t_kernel(
                 return gates_io[g][:, BANK * t : BANK * (t + 1)]
             return gates_u[g][:, BANK * second : BANK * (second + 1)]
 
-        def vector_bank(n):
+        def vector_empty(n):
             pair, k = divmod(n, 6)
             if k == 2 and tensor_bias(pair):
                 return
@@ -234,7 +238,7 @@ def tile_treelstm_pb_t_kernel(
                 other = bias_all[:, 0:BANK] if k < 2 else bias_all[:, BANK : 2 * BANK]
             nc.vector.tensor_tensor(out=dst, in0=sums[n][:], in1=other, op=ALU.add)
 
-        def scalar_bank(pair):
+        def scalar_empty(pair):
             nc.scalar.copy(out=gate_slice(pair, 2), in_=sums[6 * pair + 2][:])
 
         def sigmoid_io(pair):
@@ -260,7 +264,9 @@ def tile_treelstm_pb_t_kernel(
             store(g, t0, t1, CH, 2 * CH)
 
         def tanh_c(g, t0, t1):
-            nc.scalar.activation(out=tanh_c_sb[g][:, t0:t1, :], in_=res[g][:, t0:t1, CH : 2 * CH], func=ACT.Tanh)
+            nc.scalar.activation(
+                out=tanh_c_sb[g][:, t0:t1, :], in_=res[g][:, t0:t1, CH : 2 * CH], func=ACT.Tanh
+            )
 
         def hidden(engine, g, t0, t1):
             io = gates_io[g][:].rearrange("p (t c) -> p t c", c=BANK)
@@ -269,20 +275,23 @@ def tile_treelstm_pb_t_kernel(
             )
 
         def store(g, t0, t1, c0, c1):
-            nc.sync.dma_start(out=out_dram[:, GROUP * g + t0 : GROUP * g + t1, c0:c1], in_=res[g][:, t0:t1, c0:c1])
+            nc.sync.dma_start(
+                out=out_dram[:, GROUP * g + t0 : GROUP * g + t1, c0:c1], in_=res[g][:, t0:t1, c0:c1]
+            )
 
         def after_pair(pair):
             g, second = divmod(pair, 2)
             if pair + 1 < PAIRS and tensor_bias(pair + 1):
-                scalar_bank(pair + 1)
+                scalar_empty(pair + 1)
             ahead = g + 2
             if not second:
-                if 3 <= ahead < GROUPS:
-                    regroup_z(ahead, 0)
+                if HEAD_GROUPS <= ahead < GROUPS:
                     regroup_z(ahead, 1)
                 return
-            if 3 <= ahead < GROUPS:
+            if HEAD_GROUPS <= ahead < GROUPS:
                 copy_h(ahead)
+            if HEAD_GROUPS <= ahead + 1 < GROUPS:
+                regroup_z(ahead + 1, 0)
             if g < GROUPS - 1:
                 cell(nc.gpsimd, g, 0, GROUP)
             if g >= 1:
@@ -309,37 +318,41 @@ def tile_treelstm_pb_t_kernel(
         bias_uu = sum_psum.tile([P, BANK], F32, name="bias_uu", tag="sum")
         for j in range(2):
             nc.tensor.matmul(
-                out=bias_uu[:, CH * j : CH * (j + 1)], lhsT=ones[:], rhs=bias_rows[:, BANK : 3 * CH], start=True, stop=True
+                out=bias_uu[:, CH * j : CH * (j + 1)],
+                lhsT=ones[:],
+                rhs=bias_rows[:, BANK : 3 * CH],
+                start=True,
+                stop=True,
             )
         nc.scalar.copy(out=bias_all[:, 0:BANK], in_=bias_io[:])
         nc.vector.tensor_copy(out=bias_all[:, BANK : 2 * BANK], in_=bias_uu[:])
 
-        def plain_bank(n):
-            tensor_bank(n)
-            vector_bank(n)
+        def plain_fill(n):
+            tensor_fill(n)
+            vector_empty(n)
 
-        plain_bank(0)
+        plain_fill(0)
         front_w(0)
-        plain_bank(1)
+        plain_fill(1)
         front_w(1)
         front_z(0, 0)
-        plain_bank(2)
+        plain_fill(2)
         quantise_w(0, BANK)
         front_w(2)
         quantise_z(0, 0, 1)
-        plain_bank(6)
+        plain_fill(6)
         quantise_w(BANK, 3 * CH)
         front_z(0, 1)
-        plain_bank(7)
+        plain_fill(7)
         quantise_z(0, 1, 2)
-        plain_bank(8)
+        plain_fill(8)
         front_h(1)
         front_z(1, 0)
         front_z(1, 1)
         for n in (3, 4, 5):
-            tensor_bank(n)
+            tensor_fill(n)
         for n in (3, 4, 5):
-            vector_bank(n)
+            vector_empty(n)
         quantise_z(1)
         front_z(2, 0)
         front_z(2, 1)
@@ -348,14 +361,13 @@ def tile_treelstm_pb_t_kernel(
         tanh_u(0)
         after_pair(0)
 
-        done = 9
-        for n in range(done, BANKS + LEAD):
-            if n < BANKS:
-                tensor_bank(n)
-            if n - LEAD < done:
+        for n in range(HEAD_FILLS, FILLS + LEAD):
+            if n < FILLS:
+                tensor_fill(n)
+            if n - LEAD < HEAD_FILLS:
                 continue
             pair, k = divmod(n - LEAD, 6)
-            vector_bank(n - LEAD)
+            vector_empty(n - LEAD)
             if k == 4:
                 sigmoid_io(pair)
             if k == 5:

@@ -24,7 +24,7 @@ RING = 5
 LEAD = RING - 1
 HEAD_GROUPS = 3
 HEAD_FILLS = 9
-FIRST_TENSOR_BIAS = 2
+FIRST_TENSOR_BIAS = 6
 GPSIMD_H = 2
 FLOPS = 2 * NODES * (SIZE + CH) * 3 * CH
 

from contextlib import ExitStack

import concourse.mybir as mybir
from concourse.masks import make_identity

F32 = mybir.dt.float32
BF16 = mybir.dt.bfloat16
U32 = mybir.dt.uint32
U8 = mybir.dt.uint8
I32 = mybir.dt.int32
FP8X4 = mybir.dt.float8_e4m3fn_x4
ACT = mybir.ActivationFunctionType
ALU = mybir.AluOpType

P = 128
NODES, SIZE, CH = 4096, 512, 256
TILES = NODES // P
GROUP = 4
GROUPS = TILES // GROUP
PAIRS = TILES // 2
BANK = 512
FILLS = 6 * PAIRS
RING = 5
LEAD = RING - 1
HEAD_GROUPS = 3
HEAD_FILLS = 9
FIRST_TENSOR_BIAS = 6
GPSIMD_H = 2
FLOPS = 2 * NODES * (SIZE + CH) * 3 * CH


def tile_treelstm_pb_t_kernel(
    tc, z0, h_tilde, fc_sum, W_i, U_i, b_i, W_o, U_o, b_o, W_u, U_u, b_u, out
):
    nc = tc.nc
    with ExitStack() as ctx:
        ctx.enter_context(tc.manual_schedule())
        keep = ctx.enter_context(tc.tile_pool(name="keep", bufs=1))
        front = ctx.enter_context(tc.tile_pool(name="front", bufs=3))
        io_pool = ctx.enter_context(tc.tile_pool(name="io", bufs=4))
        u_pool = ctx.enter_context(tc.tile_pool(name="u", bufs=3))
        res_pool = ctx.enter_context(tc.tile_pool(name="res", bufs=4))
        tanh_pool = ctx.enter_context(tc.tile_pool(name="tanh", bufs=3))
        turn_psum = ctx.enter_context(tc.psum_pool(name="turn", bufs=8 - RING))
        sum_psum = ctx.enter_context(tc.psum_pool(name="sums", bufs=RING))

        z_dram = z0.rearrange("(p t) k -> p t k", t=TILES)
        h_dram = h_tilde.rearrange("(p t) k -> p t k", t=TILES)
        fc_dram = fc_sum.rearrange("(p t) k -> p t k", t=TILES)
        out_dram = out.rearrange("(p t) c -> p t c", t=TILES)

        bias_rows = keep.tile([P, 3 * CH], BF16, name="bias_rows")
        nc.vector.memset(bias_rows[:].bitcast(I32), 0)
        for j, b in enumerate((b_i, b_o, b_u)):
            nc.scalar.dma_start(
                out=bias_rows[0:1, CH * j : CH * (j + 1)], in_=b.rearrange("(o n) -> o n", o=1)
            )
        identity = keep.tile([P, P], F32, name="identity")
        make_identity(nc, identity[:])
        ones = keep.tile([P, P], BF16, name="ones")
        nc.vector.memset(ones[:], 1.0)
        warm = keep.tile([P, 8], F32, name="warm")
        nc.vector.memset(warm[:], 0.0)
        nc.scalar.activation(out=warm[:], in_=warm[:], func=ACT.Sigmoid)

        z_in = [keep.tile([P, GROUP, SIZE], BF16, name="z_in%d" % g) for g in range(GROUPS)]
        h_in = [keep.tile([P, GROUP, CH], BF16, name="h_in%d" % g) for g in range(GROUPS)]
        fc_in = [keep.tile([P, GROUP, CH], BF16, name="fc_in%d" % g) for g in range(GROUPS)]
        w_in = [keep.tile([P, 2, SIZE], BF16, name="w_in%d" % j) for j in range(3)]
        u_in = [keep.tile([P, 2, CH], BF16, name="u_in%d" % j) for j in range(3)]

        def load(dst, src, g, t0=0, t1=GROUP):
            nc.sync.dma_start(out=dst[g][:, t0:t1, :], in_=src[:, GROUP * g + t0 : GROUP * g + t1, :])

        def load_weight(dst, src):
            nc.sync.dma_start(out=dst[:], in_=src.rearrange("(b p) k -> p b k", p=P))

        load_weight(u_in[0], U_i)
        load_weight(u_in[1], U_o)
        load(h_in, h_dram, 0)
        load_weight(u_in[2], U_u)
        load_weight(w_in[0], W_i)
        load_weight(w_in[1], W_o)
        load(z_in, z_dram, 0, 0, 2)
        load_weight(w_in[2], W_u)
        load(z_in, z_dram, 0, 2, 4)
        for g in range(1, GROUPS):
            load(z_in, z_dram, g)
            load(h_in, h_dram, g)
            if g >= 2:
                load(fc_in, fc_dram, g - 2)
        load(fc_in, fc_dram, GROUPS - 2)
        load(fc_in, fc_dram, GROUPS - 1)

        def words(tile_ap):
            return tile_ap[:].rearrange("p a k -> p (a k)").bitcast(F32)

        def turn(bank, at, src_words, square):
            nc.tensor.transpose(
                bank[:, P * at : P * (at + 1)], src_words[:, P * square : P * (square + 1)], identity[:]
            )

        h_bank, z_bank = {}, {}

        def turn_h(g, j):
            if j == 0:
                h_bank[g] = turn_psum.tile([P, BANK], F32, name="h_bank%d" % g, tag="turn")
            turn(h_bank[g], j, words(h_in[g]), j)

        def turn_z(g, half, j):
            if j == 0:
                z_bank[g, half] = turn_psum.tile([P, BANK], F32, name="z_bank%d_%d" % (g, half), tag="turn")
            turn(z_bank[g, half], j, words(z_in[g]), 4 * half + j)

        def regroup(dst_words, bank):
            nc.scalar.copy(
                out=dst_words.rearrange("p (s m v) -> p s m v", s=2, m=P, v=2),
                in_=bank[:].rearrange("p (s v m) -> p s m v", s=2, v=2, m=P),
            )

        hT, z_grouped, z_codes, z_scales = {}, {}, {}, {}

        def copy_h(g):
            hT[g] = front.tile([P, BANK], F32, name="hT%d" % g, tag="hT")
            nc.scalar.copy(out=hT[g][:], in_=h_bank[g][:])

        def regroup_z(g, half):
            if half == 0:
                z_grouped[g] = front.tile(
                    [P, 4 * BANK], BF16, name="z_grouped%d" % g, tag="zg", align_bytes=64
                )
            regroup(z_grouped[g][:].bitcast(F32)[:, BANK * half : BANK * (half + 1)], z_bank[g, half])

        def quantise_z(g, half0=0, half1=2):
            if half0 == 0:
                z_codes[g] = front.tile([P, BANK], U32, name="z_codes%d" % g, tag="zc", align_bytes=64)
                z_scales[g] = front.tile([P, BANK], U8, name="z_scales%d" % g, tag="zs", align_bytes=64)
            nc.vector.quantize_mx(
                out=z_codes[g][:, 2 * P * half0 : 2 * P * half1].bitcast(FP8X4),
                scales=z_scales[g][:, 2 * P * half0 : 2 * P * half1],
                in_=z_grouped[g][:, 8 * P * half0 : 8 * P * half1],
            )

        def front_h(g):
            for j in range(GROUP):
                turn_h(g, j)
            copy_h(g)

        def front_z(g, half):
            for j in range(4):
                turn_z(g, half, j)
            regroup_z(g, half)

        def ride(pair, j):
            g = pair // 2 + 2
            if HEAD_GROUPS <= g < GROUPS:
                turn_z(g, pair % 2, j)
                if pair % 2 == 1:
                    turn_h(g, j)

        uT_words = keep.tile([P, 3 * CH], F32, name="uT_words")
        uT = uT_words[:].bitcast(BF16).rearrange("p (n e) -> p n e", e=2)
        bias_all = keep.tile([P, 2 * BANK], F32, name="bias_all")
        w_grouped = keep.tile([P, 12 * CH], BF16, name="w_grouped", align_bytes=64)
        w_codes = keep.tile([P, 3 * CH], U32, name="w_codes", align_bytes=64)
        w_scales = keep.tile([P, 3 * CH], U8, name="w_scales", align_bytes=64)

        def front_w(j):
            bank = sum_psum.tile([P, BANK], F32, name="w_bank%d" % j, tag="sum")
            for square in range(4):
                turn(bank, square, words(w_in[j]), square)
            regroup(w_grouped[:].bitcast(F32)[:, BANK * j : BANK * (j + 1)], bank)

        def quantise_w(c0, c1):
            nc.vector.quantize_mx(
                out=w_codes[:, c0:c1].bitcast(FP8X4), scales=w_scales[:, c0:c1], in_=w_grouped[:, 4 * c0 : 4 * c1]
            )

        sums, gates_io, gates_u = {}, {}, {}

        def tensor_bias(pair):
            return pair >= FIRST_TENSOR_BIAS

        def tensor_fill(n):
            pair, k = divmod(n, 6)
            g, second = divmod(pair, 2)
            sums[n] = sum_psum.tile([P, BANK], F32, name="sums%d" % n, tag="sum")
            if k % 3 < 2:
                parts = [(2 * second + k % 3, 0, BANK, 0)]
            else:
                parts = [(2 * second, BANK, 3 * CH, 0), (2 * second + 1, BANK, 3 * CH, CH)]
            for t, c0, c1, at in parts:
                dst = sums[n][:, at : at + c1 - c0]
                if k >= 3:
                    nc.tensor.matmul_mx(
                        out=dst,
                        lhsT=z_codes[g][:, P * t : P * (t + 1)].bitcast(FP8X4),
                        lhsT_scale=z_scales[g][:, P * t : P * (t + 1)],
                        rhs=w_codes[:, c0:c1].bitcast(FP8X4),
                        rhs_scale=w_scales[:, c0:c1],
                        start=True,
                        stop=True,
                    )
                    continue
                h_tile = hT[g][:].bitcast(BF16).rearrange("p (t m e) -> p t m e", t=GROUP, m=P, e=2)
                with_bias = k == 2 and tensor_bias(pair)
                for e in range(2):
                    nc.tensor.matmul(
                        out=dst,
                        lhsT=h_tile[:, t, :, e],
                        rhs=uT[:, c0:c1, e],
                        start=(e == 0),
                        stop=(e == 1 and not with_bias),
                    )
                    if k < 2:
                        ride(pair, 2 * k + e)
                if with_bias:
                    nc.tensor.matmul(out=dst, lhsT=ones[:], rhs=bias_rows[:, c0:c1], start=False, stop=True)

        def gate_slice(pair, k):
            g, second = divmod(pair, 2)
            if g not in gates_io:
                gates_io[g] = io_pool.tile([P, GROUP * BANK], F32, name="gates_io%d" % g, tag="io")
                gates_u[g] = u_pool.tile([P, GROUP * CH], F32, name="gates_u%d" % g, tag="u")
            if k % 3 < 2:
                t = 2 * second + k % 3
                return gates_io[g][:, BANK * t : BANK * (t + 1)]
            return gates_u[g][:, BANK * second : BANK * (second + 1)]

        def vector_empty(n):
            pair, k = divmod(n, 6)
            if k == 2 and tensor_bias(pair):
                return
            dst = gate_slice(pair, k)
            if k >= 3:
                other = dst
            else:
                other = bias_all[:, 0:BANK] if k < 2 else bias_all[:, BANK : 2 * BANK]
            nc.vector.tensor_tensor(out=dst, in0=sums[n][:], in1=other, op=ALU.add)

        def scalar_empty(pair):
            nc.scalar.copy(out=gate_slice(pair, 2), in_=sums[6 * pair + 2][:])

        def sigmoid_io(pair):
            g, second = divmod(pair, 2)
            v = gates_io[g][:, 2 * BANK * second : 2 * BANK * (second + 1)]
            nc.scalar.activation(out=v, in_=v, func=ACT.Sigmoid)

        def tanh_u(pair):
            v = gate_slice(pair, 2)
            nc.scalar.activation(out=v, in_=v, func=ACT.Tanh)

        res, tanh_c_sb = {}, {}

        def cell(engine, g, t0, t1):
            if g not in res:
                res[g] = res_pool.tile([P, GROUP, 2 * CH], F32, name="res%d" % g, tag="res")
                tanh_c_sb[g] = tanh_pool.tile([P, GROUP, CH], F32, name="tanh_c%d" % g, tag="tanh")
            io = gates_io[g][:].rearrange("p (t c) -> p t c", c=BANK)
            uu = gates_u[g][:].rearrange("p (t c) -> p t c", c=CH)
            c = res[g][:, t0:t1, CH : 2 * CH]
            engine.tensor_tensor(out=c, in0=io[:, t0:t1, 0:CH], in1=uu[:, t0:t1, :], op=ALU.mult)
            engine.tensor_tensor(out=c, in0=c, in1=fc_in[g][:, t0:t1, :], op=ALU.add)
            store(g, t0, t1, CH, 2 * CH)

        def tanh_c(g, t0, t1):
            nc.scalar.activation(
                out=tanh_c_sb[g][:, t0:t1, :], in_=res[g][:, t0:t1, CH : 2 * CH], func=ACT.Tanh
            )

        def hidden(engine, g, t0, t1):
            io = gates_io[g][:].rearrange("p (t c) -> p t c", c=BANK)
            engine.tensor_tensor(
                out=res[g][:, t0:t1, 0:CH], in0=io[:, t0:t1, CH:BANK], in1=tanh_c_sb[g][:, t0:t1, :], op=ALU.mult
            )

        def store(g, t0, t1, c0, c1):
            nc.sync.dma_start(
                out=out_dram[:, GROUP * g + t0 : GROUP * g + t1, c0:c1], in_=res[g][:, t0:t1, c0:c1]
            )

        def after_pair(pair):
            g, second = divmod(pair, 2)
            if pair + 1 < PAIRS and tensor_bias(pair + 1):
                scalar_empty(pair + 1)
            ahead = g + 2
            if not second:
                if HEAD_GROUPS <= ahead < GROUPS:
                    regroup_z(ahead, 1)
                return
            if HEAD_GROUPS <= ahead < GROUPS:
                copy_h(ahead)
            if HEAD_GROUPS <= ahead + 1 < GROUPS:
                regroup_z(ahead + 1, 0)
            if g < GROUPS - 1:
                cell(nc.gpsimd, g, 0, GROUP)
            if g >= 1:
                tanh_c(g - 1, 0, GROUP)
                if g < GROUPS - 1:
                    hidden(nc.gpsimd, g - 1, 0, GPSIMD_H)
            if ahead < GROUPS:
                quantise_z(ahead)
            if g >= 2:
                hidden(nc.vector, g - 2, GPSIMD_H, GROUP)
                store(g - 2, 0, GROUP, 0, CH)

        u_bank = [sum_psum.tile([P, BANK], F32, name="u_bank%d" % j, tag="sum") for j in range(2)]
        for j in range(2):
            for b in range(2):
                turn(u_bank[0], 2 * j + b, words(u_in[j]), b)
        nc.vector.tensor_copy(out=uT_words[:, 0:BANK], in_=u_bank[0][:])
        front_h(0)
        for b in range(2):
            turn(u_bank[1], b, words(u_in[2]), b)
        nc.vector.tensor_copy(out=uT_words[:, BANK : 3 * CH], in_=u_bank[1][:, 0:CH])
        bias_io = sum_psum.tile([P, BANK], F32, name="bias_io", tag="sum")
        nc.tensor.matmul(out=bias_io[:], lhsT=ones[:], rhs=bias_rows[:, 0:BANK], start=True, stop=True)
        bias_uu = sum_psum.tile([P, BANK], F32, name="bias_uu", tag="sum")
        for j in range(2):
            nc.tensor.matmul(
                out=bias_uu[:, CH * j : CH * (j + 1)],
                lhsT=ones[:],
                rhs=bias_rows[:, BANK : 3 * CH],
                start=True,
                stop=True,
            )
        nc.scalar.copy(out=bias_all[:, 0:BANK], in_=bias_io[:])
        nc.vector.tensor_copy(out=bias_all[:, BANK : 2 * BANK], in_=bias_uu[:])

        def plain_fill(n):
            tensor_fill(n)
            vector_empty(n)

        plain_fill(0)
        front_w(0)
        plain_fill(1)
        front_w(1)
        front_z(0, 0)
        plain_fill(2)
        quantise_w(0, BANK)
        front_w(2)
        quantise_z(0, 0, 1)
        plain_fill(6)
        quantise_w(BANK, 3 * CH)
        front_z(0, 1)
        plain_fill(7)
        quantise_z(0, 1, 2)
        plain_fill(8)
        front_h(1)
        front_z(1, 0)
        front_z(1, 1)
        for n in (3, 4, 5):
            tensor_fill(n)
        for n in (3, 4, 5):
            vector_empty(n)
        quantise_z(1)
        front_z(2, 0)
        front_z(2, 1)
        front_h(2)
        sigmoid_io(0)
        tanh_u(0)
        after_pair(0)

        for n in range(HEAD_FILLS, FILLS + LEAD):
            if n < FILLS:
                tensor_fill(n)
            if n - LEAD < HEAD_FILLS:
                continue
            pair, k = divmod(n - LEAD, 6)
            vector_empty(n - LEAD)
            if k == 4:
                sigmoid_io(pair)
            if k == 5:
                tanh_u(pair)
                after_pair(pair)

        last = GROUPS - 1
        for t0 in (0, 2):
            cell(nc.vector, last, t0, t0 + 2)
            tanh_c(last, t0, t0 + 2)
        hidden(nc.vector, last - 1, 0, GROUP)
        store(last - 1, 0, GROUP, 0, CH)
        for t0 in (0, 2):
            hidden(nc.vector, last, t0, t0 + 2)
            store(last, t0, t0 + 2, 0, CH)
